import numpy as np
import ml_dtypes


def mxq(x, axis, fmt="e4m3"):
    dtype, down = {"e4m3": (ml_dtypes.float8_e4m3fn, 7), "e5m2": (ml_dtypes.float8_e5m2, 14)}[fmt]
    v = np.moveaxis(np.asarray(x, np.float32).astype(ml_dtypes.bfloat16).astype(np.float64), axis, -1)
    blocks = v.reshape(v.shape[:-1] + (-1, 32))
    amax = np.abs(blocks).max(-1, keepdims=True)
    byte = np.maximum(np.where(amax > 0, np.frexp(amax)[1] - 1 + 127, 0) - down, 1)
    scale = np.exp2(byte - 127.0)
    codes = (blocks / scale).astype(np.float32).astype(dtype).astype(np.float64)
    return np.moveaxis((codes * scale).reshape(v.shape), -1, axis)


WIDE = False


def mx_kscale(k):
    if not WIDE:
        return np.ones(k)
    levels = np.array([10, -10, 5, -5, 0])
    if k % 512:
        return np.exp2(np.random.permutation(np.resize(levels, k // 32))).repeat(32)
    a = np.empty((k // 512, 16))
    for p in range(k // 512):
        a[p, :8] = np.random.permutation(np.resize(levels, 8))
        for g in range(8):
            far = levels[np.abs(levels - a[p, g]) >= 10]
            a[p, g + 8] = far[np.random.randint(len(far))]
    return np.exp2(a.ravel()).repeat(32)


BF16 = ml_dtypes.bfloat16


def bf(x):
    return np.asarray(x, np.float32).astype(BF16)


def f64(x):
    return np.asarray(x).astype(np.float64)


B, T, I, H = 128, 8, 1024, 1024


def sigmoid(v):
    return 1.0 / (1.0 + np.exp(-v))


def setup_inputs():
    s = mx_kscale(I)
    d = {"inputs": bf(np.random.standard_normal((B, T, I)) * s),
         "h0": bf(np.random.standard_normal((1, B, H))),
         "c0": bf(np.random.standard_normal((1, B, H)))}
    for ni, nh in (("ii", "hi"), ("if_", "hf"), ("io", "ho"), ("ig", "hg")):
        d["w_" + ni] = bf(np.random.standard_normal((H, I)) / np.sqrt(I) / s[None, :])
        d["b_" + ni] = bf(np.random.standard_normal((H, 1)) * 0.3)
        d["w_" + nh] = bf(np.random.standard_normal((H, H)) * 0.7 / np.sqrt(H))
        d["b_" + nh] = bf(np.random.standard_normal((H, 1)) * 0.3)
    return d


def reference(inputs, h0, c0, w_ii, b_ii, w_hi, b_hi, w_if_, b_if_, w_hf, b_hf, w_io, b_io, w_ho, b_ho, w_ig, b_ig, w_hg, b_hg):
    xq = mxq(f64(inputs), 2, "e4m3")
    h0s = f64(h0)[0]
    c0s = f64(c0)[0]
    zi = (xq @ mxq(f64(w_ii), 1, "e4m3").T) + (h0s @ f64(w_hi).T)[:, None, :] + f64(b_ii)[:, 0] + f64(b_hi)[:, 0]
    zf = (xq @ mxq(f64(w_if_), 1, "e4m3").T) + (h0s @ f64(w_hf).T)[:, None, :] + f64(b_if_)[:, 0] + f64(b_hf)[:, 0]
    zg = (xq @ mxq(f64(w_ig), 1, "e4m3").T) + (h0s @ f64(w_hg).T)[:, None, :] + f64(b_ig)[:, 0] + f64(b_hg)[:, 0]
    zo = (xq @ mxq(f64(w_io), 1, "e4m3").T) + (h0s @ f64(w_ho).T)[:, None, :] + f64(b_io)[:, 0] + f64(b_ho)[:, 0]
    i = sigmoid(zi)
    f = sigmoid(zf)
    g = np.tanh(zg)
    o = sigmoid(zo)
    c_next = f * c0s[:, None, :] + i * g
    h_next = o * np.tanh(c_next)
    hidden_seq = np.transpose(h_next, (1, 0, 2))
    h_last = hidden_seq[-1][None]
    c_last = c_next[:, -1][None]
    return hidden_seq, h_last, c_last

@@ -1,0 +1,327 @@
+from contextlib import ExitStack
+
+import concourse.mybir as mybir
+from concourse.masks import make_identity
+
+F32 = mybir.dt.float32
+BF16 = mybir.dt.bfloat16
+U32 = mybir.dt.uint32
+U8 = mybir.dt.uint8
+I32 = mybir.dt.int32
+FP8X4 = mybir.dt.float8_e4m3fn_x4
+ACT = mybir.ActivationFunctionType
+ALU = mybir.AluOpType
+
+P = 128
+B, T, I, H = 128, 8, 1024, 1024
+NG = 4
+NCH = H // P
+NT = 4
+RAW_BUFS = 24
+PINNED = True
+NU = 2 * NCH
+TAIL_V = 2
+PRODUCTS = (0, 1, 1)
+COPY_X = (0, 1)
+COPY_I = (0, 0, 1, 1)
+COPY_H = (1, 1, 1, 1)
+COPY_G = 1
+
+FLOPS = 2 * B * T * I * NG * H + 2 * B * H * NG * H
+
+
+def tile_naivelstm_pa_kernel(
+    tc,
+    inputs, h0, c0,
+    w_ii, b_ii, w_hi, b_hi,
+    w_if_, b_if_, w_hf, b_hf,
+    w_io, b_io, w_ho, b_ho,
+    w_ig, b_ig, w_hg, b_hg,
+    out_0, out_1, out_2,
+):
+    nc = tc.nc
+    w_in = [w_ii, w_if_, w_io, w_ig]
+    w_hid = [w_hi, w_hf, w_ho, w_hg]
+    b_in = [b_ii, b_if_, b_io, b_ig]
+    b_hid = [b_hi, b_hf, b_ho, b_hg]
+
+    with ExitStack() as ctx:
+        if PINNED:
+            ctx.enter_context(tc.manual_schedule())
+        const = ctx.enter_context(tc.tile_pool(name="const", bufs=1))
+        raw = ctx.enter_context(tc.tile_pool(name="raw", bufs=RAW_BUFS))
+        wgp = ctx.enter_context(tc.tile_pool(name="wgp", bufs=2))
+        wqp = ctx.enter_context(tc.tile_pool(name="wqp", bufs=3))
+        whp = ctx.enter_context(tc.tile_pool(name="whp", bufs=2))
+        zp = ctx.enter_context(tc.tile_pool(name="zp", bufs=4))
+        hp = ctx.enter_context(tc.tile_pool(name="hp", bufs=3))
+        psum = ctx.enter_context(tc.psum_pool(name="psum", bufs=8))
+
+        ident = const.tile([P, P], F32, name="ident")
+        ones = const.tile([P, P], BF16, name="ones")
+        scratch = const.tile([P, 1], F32, name="scratch")
+        bias_sb = const.tile([P, NCH, NG, P], BF16, name="bias_sb")
+        h0_raw = const.tile([P, H], BF16, name="h0_raw")
+        c0_sb = const.tile([P, H], BF16, name="c0_sb")
+        h_t = const.tile([P, 4, 2, P], BF16, name="h_t")
+        x_raw = const.tile([P, T, I], BF16, name="x_raw")
+        xg = const.tile([P, T, I], BF16, name="xg", align_bytes=64)
+        xq = const.tile([P, T, I // 4], U32, name="xq", align_bytes=64)
+        xs = const.tile([P, T, I // 4], U8, name="xs", align_bytes=64)
+        gsum = const.tile([P, NCH, NG * P], F32, name="gsum")
+
+        make_identity(nc, ident[:])
+        nc.vector.memset(scratch[:], 0.0)
+        nc.scalar.activation(out=scratch[:], in_=scratch[:], func=ACT.Sigmoid)
+        nc.vector.memset(ones[:], 1.0)
+        nc.vector.memset(bias_sb[:].bitcast(I32), 0)
+
+        plan = [
+            ("h0", 0), ("H", 0), ("x", 0), ("hid", 0), ("x", 1), ("I", 0),
+            ("x", 2), ("x", 3), ("H", 1), ("U", 0), ("U", 1), ("I", 1), ("hid", 1), ("H", 2),
+        ]
+        for u in range(2, NU):
+            k, half = divmod(u, 2)
+            plan.append(("U", u))
+            if half == 0 and k + 1 < NCH:
+                plan.extend([("I", k + 1), ("hid", k + 1)])
+            elif half == 1 and k + 2 < NCH:
+                plan.append(("H", k + 2))
+
+        blocks = []
+        for kind, k in plan:
+            if kind == "H" or kind == "I":
+                blocks.extend([(kind, k, g) for g in range(NG)])
+        raw_tiles = {}
+        cursor = [0]
+
+        def issue_load():
+            n = cursor[0]
+            if n < len(blocks):
+                kind, k, g = blocks[n]
+                w = w_hid[g] if kind == "H" else w_in[g]
+                wraw = raw.tile([P, I], BF16, name="wraw", tag="wraw")
+                nc.sync.dma_start(out=wraw[:], in_=w[k * P:(k + 1) * P, :])
+                raw_tiles[blocks[n]] = wraw
+                cursor[0] = n + 1
+
+        for kind, k in plan:
+            if kind == "h0":
+                nc.sync.dma_start(out=h0_raw[:], in_=h0[0])
+            elif kind == "x":
+                nc.sync.dma_start(
+                    out=x_raw[:, 2 * k:2 * k + 2, :], in_=inputs[:, 2 * k:2 * k + 2, :]
+                )
+            elif (kind == "H" or kind == "I") and cursor[0] < RAW_BUFS:
+                for g in range(NG):
+                    issue_load()
+        for g in range(NG):
+            nc.scalar.dma_start(
+                out=bias_sb[0:1, :, g, :],
+                in_=b_in[g].rearrange("(k r) o -> o k r", r=P),
+            )
+            nc.scalar.dma_start(
+                out=bias_sb[1:2, :, g, :],
+                in_=b_hid[g].rearrange("(k r) o -> o k r", r=P),
+            )
+        nc.scalar.dma_start(out=c0_sb[:], in_=c0[0])
+
+        def copy(engine, out, in_):
+            if engine == 0:
+                nc.vector.tensor_copy(out=out, in_=in_)
+            else:
+                nc.scalar.copy(out=out, in_=in_)
+
+        def transpose_words(words):
+            bank = psum.tile([P, 4, P], F32, name="tp", tag="bank")
+            for q in range(4):
+                nc.tensor.transpose(bank[:, q, :], words[:, q * P:(q + 1) * P], ident[:])
+            return bank
+
+        def transpose_for_mx(words):
+            bank = psum.tile([P, 4, P], F32, name="tp", tag="bank")
+            for g in range(2):
+                for u in range(2):
+                    nc.tensor.transpose(
+                        bank[:, 2 * g + u, :], words[:, 256 * g + u:256 * (g + 1):2], ident[:]
+                    )
+            return bank
+
+        def regrouped(bank):
+            return bank[:].rearrange("p (g u) r -> p g r u", u=2)
+
+        wh_tiles = {}
+        wg_tiles = {}
+        wq_tiles = {}
+        z_tiles = {}
+        state = {"late": None, "pending": []}
+
+        def flush_pending():
+            todo = state["pending"]
+            state["pending"] = []
+            for f in todo:
+                f()
+
+        def run_late():
+            f = state["late"]
+            state["late"] = None
+            if f is not None:
+                f()
+
+        def quantise_x(pair):
+            tt = slice(2 * pair, 2 * pair + 2)
+            nc.vector.quantize_mx(
+                out=xq[:, tt, :].rearrange("p t c -> p (t c)").bitcast(FP8X4),
+                scales=xs[:, tt, :].rearrange("p t c -> p (t c)"),
+                in_=xg[:, tt, :].rearrange("p t c -> p (t c)"),
+            )
+
+        def quantise_w(k):
+            wg = wg_tiles[k]
+            wq = wqp.tile([P, 2, NG * P], U32, name="wq", align_bytes=64)
+            ws = wqp.tile([P, 2, NG * P], U8, name="ws", align_bytes=64)
+            wq_tiles[k] = (wq, ws)
+            nc.vector.quantize_mx(
+                out=wq[:].rearrange("p g c -> p (g c)").bitcast(FP8X4),
+                scales=ws[:].rearrange("p g c -> p (g c)"),
+                in_=wg[:].rearrange("p g n c -> p (g n c)"),
+            )
+
+        def product(engine, out, in0, in1, op):
+            if engine == 0:
+                nc.vector.tensor_tensor(out=out, in0=in0, in1=in1, op=op)
+            else:
+                nc.gpsimd.tensor_tensor(out=out, in0=in0, in1=in1, op=op)
+
+        def finish(u):
+            k, half = divmod(u, 2)
+            ks = slice(k * P, (k + 1) * P)
+            z = z_tiles[u]
+            hout = hp.tile([P, NT, P], F32, name="hout")
+            nc.vector.tensor_tensor(out=hout[:], in0=z[:, 2], in1=z[:, 1], op=ALU.mult)
+            t0 = half * NT
+            nc.sync.dma_start(
+                out=out_0[t0:t0 + NT, :, ks].rearrange("t b h -> b t h"), in_=hout[:]
+            )
+            if half == 1:
+                nc.sync.dma_start(out=out_1[0, :, ks], in_=hout[:, NT - 1, :])
+                nc.sync.dma_start(out=out_2[0, :, ks], in_=z[:, 3, NT - 1, :])
+
+        def elementwise(s):
+            a = s - 1
+            if 0 <= a < NU:
+                z = z_tiles[a]
+                k = a // 2
+                eng = (0, 0, 0) if a >= NU - TAIL_V else PRODUCTS
+                sig = z[:, 0:3, :, :].rearrange("p g t r -> p (g t r)")
+                nc.scalar.activation(out=sig, in_=sig, func=ACT.Sigmoid)
+                product(
+                    eng[0], z[:, 1], z[:, 1],
+                    c0_sb[:, k * P:(k + 1) * P].unsqueeze(1).to_broadcast([P, NT, P]),
+                    ALU.mult,
+                )
+                nc.scalar.activation(out=z[:, 3], in_=z[:, 3], func=ACT.Tanh)
+                product(eng[1], z[:, 0], z[:, 0], z[:, 3], ALU.mult)
+                product(eng[2], z[:, 3], z[:, 0], z[:, 1], ALU.add)
+            b = s - 2
+            if 0 <= b < NU:
+                z = z_tiles[b]
+                nc.scalar.activation(out=z[:, 1], in_=z[:, 3], func=ACT.Tanh)
+                state["late"] = lambda: finish(b)
+
+        for kind, k in plan:
+            if kind == "h0":
+                bank = transpose_words(h0_raw[:].bitcast(F32))
+                nc.vector.tensor_copy(
+                    out=h_t[:],
+                    in_=bank[:].bitcast(BF16).rearrange("p j (b e) -> p j e b", e=2),
+                )
+            elif kind == "x":
+                banks = [
+                    transpose_for_mx(x_raw[:].bitcast(F32)[:, t, :]) for t in (2 * k, 2 * k + 1)
+                ]
+                for n in range(2):
+                    copy(
+                        COPY_X[n],
+                        xg[:].bitcast(F32)[:, 2 * k + n, :].rearrange(
+                            "p (g r u) -> p g r u", g=2, u=2
+                        ),
+                        regrouped(banks[n]),
+                    )
+                flush_pending()
+                state["pending"].append(lambda pair=k: quantise_x(pair))
+            elif kind == "H":
+                wh_t = whp.tile([P, 4, NG * P], F32, name="wh_t")
+                wh_tiles[k] = wh_t
+                banks = []
+                for g in range(NG):
+                    banks.append(transpose_words(raw_tiles[("H", k, g)][:].bitcast(F32)))
+                    issue_load()
+                for g in range(NG):
+                    copy((1, 0, 1, 0)[g] if k == 0 else COPY_H[g], wh_t[:, :, g * P:(g + 1) * P], banks[g][:])
+                flush_pending()
+                run_late()
+            elif kind == "I":
+                wg = wgp.tile([P, 2, NG, 4 * P], BF16, name="wg", align_bytes=64)
+                wg_tiles[k] = wg
+                banks = []
+                for g in range(NG):
+                    banks.append(transpose_for_mx(raw_tiles[("I", k, g)][:].bitcast(F32)))
+                    issue_load()
+                for g in range(NG):
+                    copy(
+                        (0, 1, 0, 1)[g] if k == 0 else COPY_I[g],
+                        wg[:].bitcast(F32)[:, :, g, :].rearrange("p g (r u) -> p g r u", u=2),
+                        regrouped(banks[g]),
+                    )
+                flush_pending()
+                run_late()
+                state["pending"].append(lambda chunk=k: quantise_w(chunk))
+            elif kind == "hid":
+                wv = wh_tiles[k][:].bitcast(BF16).rearrange("p j (c e) -> p j c e", e=2)
+                bank = psum.tile([P, NG * P], F32, name="hid", tag="bank")
+                for j in range(4):
+                    for e in range(2):
+                        nc.tensor.matmul(
+                            bank[:], lhsT=h_t[:, j, e, :], rhs=wv[:, j, :, e],
+                            start=(j == 0 and e == 0), stop=False,
+                        )
+                nc.tensor.matmul(
+                    bank[:], lhsT=ones[:],
+                    rhs=bias_sb[:, k, :, :].rearrange("p g r -> p (g r)"),
+                    start=False, stop=True,
+                )
+                flush_pending()
+                copy(COPY_G, gsum[:, k, :], bank[:])
+            else:
+                flush_pending()
+                run_late()
+                chunk, half = divmod(k, 2)
+                wq, ws = wq_tiles[chunk]
+                z = zp.tile([P, NG, NT, P], F32, name="z")
+                z_tiles[k] = z
+                for tl in range(NT):
+                    t = half * NT + tl
+                    bank = psum.tile([P, NG, P], F32, name="mx", tag="bank")
+                    for g in range(2):
+                        cols = slice(g * P, (g + 1) * P)
+                        nc.tensor.matmul_mx(
+                            out=bank[:].rearrange("p g r -> p (g r)"),
+                            lhsT=xq[:, t, cols].bitcast(FP8X4),
+                            lhsT_scale=xs[:, t, cols],
+                            rhs=wq[:, g, :].bitcast(FP8X4),
+                            rhs_scale=ws[:, g, :],
+                            start=(g == 0),
+                            stop=(g == 1),
+                        )
+                    nc.vector.tensor_tensor(
+                        out=z[:, :, tl, :],
+                        in0=bank[:],
+                        in1=gsum[:, chunk, :].rearrange("p (g r) -> p g r", g=NG),
+                        op=ALU.add,
+                    )
+                elementwise(k)
+        run_late()
+        for s in range(NU, NU + 2):
+            elementwise(s)
+            run_late()

@@ -21,9 +21,8 @@ RAW_BUFS = 24
 PINNED = True
 NU = 2 * NCH
 TAIL_V = 2
-PRODUCTS = (0, 1, 1)
 COPY_X = (0, 1)
-COPY_I = (0, 0, 1, 1)
+COPY_I = (0, 0, 1, 0)
 COPY_H = (1, 1, 1, 1)
 COPY_G = 1
 
@@ -55,9 +54,11 @@ def tile_naivelstm_pa_kernel(
         whp = ctx.enter_context(tc.tile_pool(name="whp", bufs=2))
         zp = ctx.enter_context(tc.tile_pool(name="zp", bufs=4))
         hp = ctx.enter_context(tc.tile_pool(name="hp", bufs=3))
-        psum = ctx.enter_context(tc.psum_pool(name="psum", bufs=8))
+        psum = ctx.enter_context(tc.psum_pool(name="psum", bufs=7))
+        psum_c0 = ctx.enter_context(tc.psum_pool(name="psum_c0", bufs=1))
 
         ident = const.tile([P, P], F32, name="ident")
+        ident_bf = const.tile([P, P], BF16, name="ident_bf")
         ones = const.tile([P, P], BF16, name="ones")
         scratch = const.tile([P, 1], F32, name="scratch")
         bias_sb = const.tile([P, NCH, NG, P], BF16, name="bias_sb")
@@ -71,6 +72,7 @@ def tile_naivelstm_pa_kernel(
         gsum = const.tile([P, NCH, NG * P], F32, name="gsum")
 
         make_identity(nc, ident[:])
+        make_identity(nc, ident_bf[:])
         nc.vector.memset(scratch[:], 0.0)
         nc.scalar.activation(out=scratch[:], in_=scratch[:], func=ACT.Sigmoid)
         nc.vector.memset(ones[:], 1.0)
@@ -198,7 +200,7 @@ def tile_naivelstm_pa_kernel(
             ks = slice(k * P, (k + 1) * P)
             z = z_tiles[u]
             hout = hp.tile([P, NT, P], F32, name="hout")
-            nc.vector.tensor_tensor(out=hout[:], in0=z[:, 2], in1=z[:, 1], op=ALU.mult)
+            product(0 if u >= NU - TAIL_V else 1, hout[:], z[:, 2], z[:, 1], ALU.mult)
             t0 = half * NT
             nc.sync.dma_start(
                 out=out_0[t0:t0 + NT, :, ks].rearrange("t b h -> b t h"), in_=hout[:]
@@ -207,22 +209,35 @@ def tile_naivelstm_pa_kernel(
                 nc.sync.dma_start(out=out_1[0, :, ks], in_=hout[:, NT - 1, :])
                 nc.sync.dma_start(out=out_2[0, :, ks], in_=z[:, 3, NT - 1, :])
 
+        c0_banks = {}
+
+        def c0_bank(k):
+            j = k // 4
+            if j not in c0_banks:
+                bank = psum_c0.tile([P, 4 * P], F32, name="c0_bank")
+                nc.tensor.matmul(
+                    bank[:], lhsT=ident_bf[:], rhs=c0_sb[:, 4 * j * P:4 * (j + 1) * P],
+                    start=True, stop=True,
+                )
+                c0_banks[j] = bank
+            return c0_banks[j][:, (k % 4) * P:(k % 4 + 1) * P]
+
         def elementwise(s):
             a = s - 1
             if 0 <= a < NU:
                 z = z_tiles[a]
                 k = a // 2
-                eng = (0, 0, 0) if a >= NU - TAIL_V else PRODUCTS
+                eng = 0 if a >= NU - TAIL_V else 1
                 sig = z[:, 0:3, :, :].rearrange("p g t r -> p (g t r)")
                 nc.scalar.activation(out=sig, in_=sig, func=ACT.Sigmoid)
-                product(
-                    eng[0], z[:, 1], z[:, 1],
-                    c0_sb[:, k * P:(k + 1) * P].unsqueeze(1).to_broadcast([P, NT, P]),
-                    ALU.mult,
+                nc.vector.tensor_tensor(
+                    out=z[:, 1], in0=z[:, 1],
+                    in1=c0_bank(k).unsqueeze(1).to_broadcast([P, NT, P]),
+                    op=ALU.mult,
                 )
                 nc.scalar.activation(out=z[:, 3], in_=z[:, 3], func=ACT.Tanh)
-                product(eng[1], z[:, 0], z[:, 0], z[:, 3], ALU.mult)
-                product(eng[2], z[:, 3], z[:, 0], z[:, 1], ALU.add)
+                product(eng, z[:, 0], z[:, 0], z[:, 3], ALU.mult)
+                product(eng, z[:, 3], z[:, 0], z[:, 1], ALU.add)
             b = s - 2
             if 0 <= b < NU:
                 z = z_tiles[b]

@@ -16,15 +16,15 @@ P = 128
 B, T, I, H = 128, 8, 1024, 1024
 NG = 4
 NCH = H // P
-NT = 4
 RAW_BUFS = 24
-PINNED = True
-NU = 2 * NCH
-TAIL_V = 2
-COPY_X = (0, 1)
-COPY_I = (0, 0, 1, 0)
-COPY_H = (1, 1, 1, 1)
-COPY_G = 1
+VECTOR, SCALAR, GPSIMD = 0, 1, 2
+COPY_X = (VECTOR, SCALAR)
+COPY_I = (VECTOR, VECTOR, VECTOR, VECTOR)
+COPY_I_HEAD = (VECTOR, SCALAR, VECTOR, SCALAR)
+COPY_H = (SCALAR, SCALAR, SCALAR, SCALAR)
+COPY_H_HEAD = (SCALAR, VECTOR, SCALAR, VECTOR)
+UNITS = [(k, t0, 4) for k in range(NCH - 1) for t0 in (0, 4)]
+TAIL = [(NCH - 1, 0, 2), (NCH - 1, 2, 2), (NCH - 1, 4, 2), (NCH - 1, 6, 2)]
 
 FLOPS = 2 * B * T * I * NG * H + 2 * B * H * NG * H
 
@@ -45,14 +45,13 @@ def tile_naivelstm_pa_kernel(
     b_hid = [b_hi, b_hf, b_ho, b_hg]
 
     with ExitStack() as ctx:
-        if PINNED:
-            ctx.enter_context(tc.manual_schedule())
+        ctx.enter_context(tc.manual_schedule())
         const = ctx.enter_context(tc.tile_pool(name="const", bufs=1))
         raw = ctx.enter_context(tc.tile_pool(name="raw", bufs=RAW_BUFS))
         wgp = ctx.enter_context(tc.tile_pool(name="wgp", bufs=2))
         wqp = ctx.enter_context(tc.tile_pool(name="wqp", bufs=3))
         whp = ctx.enter_context(tc.tile_pool(name="whp", bufs=2))
-        zp = ctx.enter_context(tc.tile_pool(name="zp", bufs=4))
+        zp = ctx.enter_context(tc.tile_pool(name="zp", bufs=5))
         hp = ctx.enter_context(tc.tile_pool(name="hp", bufs=3))
         psum = ctx.enter_context(tc.psum_pool(name="psum", bufs=7))
         psum_c0 = ctx.enter_context(tc.psum_pool(name="psum_c0", bufs=1))
@@ -71,65 +70,55 @@ def tile_naivelstm_pa_kernel(
         xs = const.tile([P, T, I // 4], U8, name="xs", align_bytes=64)
         gsum = const.tile([P, NCH, NG * P], F32, name="gsum")
 
-        make_identity(nc, ident[:])
-        make_identity(nc, ident_bf[:])
-        nc.vector.memset(scratch[:], 0.0)
-        nc.scalar.activation(out=scratch[:], in_=scratch[:], func=ACT.Sigmoid)
-        nc.vector.memset(ones[:], 1.0)
         nc.vector.memset(bias_sb[:].bitcast(I32), 0)
+        make_identity(nc, ident[:])
+        nc.vector.memset(scratch[:], 0.0)
+        nc.vector.memset(ones[:], 1.0)
 
-        plan = [
-            ("h0", 0), ("H", 0), ("x", 0), ("hid", 0), ("x", 1), ("I", 0),
-            ("x", 2), ("x", 3), ("H", 1), ("U", 0), ("U", 1), ("I", 1), ("hid", 1), ("H", 2),
-        ]
-        for u in range(2, NU):
-            k, half = divmod(u, 2)
-            plan.append(("U", u))
-            if half == 0 and k + 1 < NCH:
-                plan.extend([("I", k + 1), ("hid", k + 1)])
-            elif half == 1 and k + 2 < NCH:
-                plan.append(("H", k + 2))
-
-        blocks = []
-        for kind, k in plan:
-            if kind == "H" or kind == "I":
-                blocks.extend([(kind, k, g) for g in range(NG)])
+        load_order = [("H", 0), ("x", 0), ("x", 1), ("x", 2), ("x", 3), ("I", 0), ("H", 1)]
+        for k in range(NCH):
+            if k + 1 < NCH:
+                load_order.append(("I", k + 1))
+            if k + 2 < NCH:
+                load_order.append(("H", k + 2))
+        weights = [(kind, k, g) for kind, k in load_order if kind != "x" for g in range(NG)]
         raw_tiles = {}
         cursor = [0]
 
         def issue_load():
             n = cursor[0]
-            if n < len(blocks):
-                kind, k, g = blocks[n]
+            if n < len(weights):
+                kind, k, g = weights[n]
                 w = w_hid[g] if kind == "H" else w_in[g]
                 wraw = raw.tile([P, I], BF16, name="wraw", tag="wraw")
                 nc.sync.dma_start(out=wraw[:], in_=w[k * P:(k + 1) * P, :])
-                raw_tiles[blocks[n]] = wraw
+                raw_tiles[weights[n]] = wraw
                 cursor[0] = n + 1
 
-        for kind, k in plan:
-            if kind == "h0":
-                nc.sync.dma_start(out=h0_raw[:], in_=h0[0])
-            elif kind == "x":
-                nc.sync.dma_start(
-                    out=x_raw[:, 2 * k:2 * k + 2, :], in_=inputs[:, 2 * k:2 * k + 2, :]
-                )
-            elif (kind == "H" or kind == "I") and cursor[0] < RAW_BUFS:
-                for g in range(NG):
-                    issue_load()
+        nc.sync.dma_start(out=h0_raw[:], in_=h0[0])
         for g in range(NG):
             nc.scalar.dma_start(
                 out=bias_sb[0:1, :, g, :],
                 in_=b_in[g].rearrange("(k r) o -> o k r", r=P),
             )
-            nc.scalar.dma_start(
+            nc.gpsimd.dma_start(
                 out=bias_sb[1:2, :, g, :],
                 in_=b_hid[g].rearrange("(k r) o -> o k r", r=P),
             )
-        nc.scalar.dma_start(out=c0_sb[:], in_=c0[0])
+        nc.scalar.activation(out=scratch[:], in_=scratch[:], func=ACT.Sigmoid)
+        nc.gpsimd.dma_start(out=c0_sb[:], in_=c0[0])
+        make_identity(nc, ident_bf[:])
+        for kind, k in load_order:
+            if kind == "x":
+                nc.sync.dma_start(
+                    out=x_raw[:, 2 * k:2 * k + 2, :], in_=inputs[:, 2 * k:2 * k + 2, :]
+                )
+            elif cursor[0] < RAW_BUFS:
+                for g in range(NG):
+                    issue_load()
 
         def copy(engine, out, in_):
-            if engine == 0:
+            if engine == VECTOR:
                 nc.vector.tensor_copy(out=out, in_=in_)
             else:
                 nc.scalar.copy(out=out, in_=in_)
@@ -155,20 +144,27 @@ def tile_naivelstm_pa_kernel(
         wh_tiles = {}
         wg_tiles = {}
         wq_tiles = {}
+        banks_of = {}
         z_tiles = {}
-        state = {"late": None, "pending": []}
+        c0_banks = {}
 
-        def flush_pending():
-            todo = state["pending"]
-            state["pending"] = []
-            for f in todo:
-                f()
+        def prepare_h0():
+            bank = transpose_words(h0_raw[:].bitcast(F32))
+            nc.vector.tensor_copy(
+                out=h_t[:],
+                in_=bank[:].bitcast(BF16).rearrange("p j (b e) -> p j e b", e=2),
+            )
 
-        def run_late():
-            f = state["late"]
-            state["late"] = None
-            if f is not None:
-                f()
+        def transpose_x(pair):
+            for n in range(2):
+                bank = transpose_for_mx(x_raw[:].bitcast(F32)[:, 2 * pair + n, :])
+                copy(
+                    COPY_X[n],
+                    xg[:].bitcast(F32)[:, 2 * pair + n, :].rearrange(
+                        "p (g r u) -> p g r u", g=2, u=2
+                    ),
+                    regrouped(bank),
+                )
 
         def quantise_x(pair):
             tt = slice(2 * pair, 2 * pair + 2)
@@ -178,165 +174,250 @@ def tile_naivelstm_pa_kernel(
                 in_=xg[:, tt, :].rearrange("p t c -> p (t c)"),
             )
 
-        def quantise_w(k):
-            wg = wg_tiles[k]
+        def transpose_hid(k):
+            banks = []
+            for g in range(NG):
+                banks.append(transpose_words(raw_tiles[("H", k, g)][:].bitcast(F32)))
+                issue_load()
+            banks_of["H"] = banks
+
+        def copy_hid(k, engines):
+            wh_t = whp.tile([P, 4, NG * P], F32, name="wh_t")
+            wh_tiles[k] = wh_t
+            for g in range(NG):
+                copy(engines[g], wh_t[:, :, g * P:(g + 1) * P], banks_of["H"][g][:])
+
+        def matmul_hid(k):
+            wv = wh_tiles[k][:].bitcast(BF16).rearrange("p j (c e) -> p j c e", e=2)
+            bank = psum.tile([P, NG * P], F32, name="hid", tag="bank")
+            for j in range(4):
+                for e in range(2):
+                    nc.tensor.matmul(
+                        bank[:], lhsT=h_t[:, j, e, :], rhs=wv[:, j, :, e],
+                        start=(j == 0 and e == 0), stop=False,
+                    )
+            nc.tensor.matmul(
+                bank[:], lhsT=ones[:],
+                rhs=bias_sb[:, k, :, :].rearrange("p g r -> p (g r)"),
+                start=False, stop=True,
+            )
+            nc.scalar.copy(out=gsum[:, k, :], in_=bank[:])
+
+        def transpose_in(k):
+            banks = []
+            for g in range(NG):
+                banks.append(transpose_for_mx(raw_tiles[("I", k, g)][:].bitcast(F32)))
+                issue_load()
+            banks_of["I"] = banks
+
+        def copy_in(k, engines):
+            wg = wgp.tile([P, 2, NG, 4 * P], BF16, name="wg", align_bytes=64)
+            wg_tiles[k] = wg
+            for g in range(NG):
+                copy(
+                    engines[g],
+                    wg[:].bitcast(F32)[:, :, g, :].rearrange("p g (r u) -> p g r u", u=2),
+                    regrouped(banks_of["I"][g]),
+                )
+
+        def quantise_in(k):
             wq = wqp.tile([P, 2, NG * P], U32, name="wq", align_bytes=64)
             ws = wqp.tile([P, 2, NG * P], U8, name="ws", align_bytes=64)
             wq_tiles[k] = (wq, ws)
             nc.vector.quantize_mx(
                 out=wq[:].rearrange("p g c -> p (g c)").bitcast(FP8X4),
                 scales=ws[:].rearrange("p g c -> p (g c)"),
-                in_=wg[:].rearrange("p g n c -> p (g n c)"),
+                in_=wg_tiles[k][:].rearrange("p g n c -> p (g n c)"),
             )
 
+        def load_c0_bank(j):
+            bank = psum_c0.tile([P, 4 * P], F32, name="c0_bank")
+            nc.tensor.matmul(
+                bank[:], lhsT=ident_bf[:], rhs=c0_sb[:, 4 * j * P:4 * (j + 1) * P],
+                start=True, stop=True,
+            )
+            c0_banks[j] = bank
+
+        def matmul_mx(u):
+            chunk, t0, nt = u
+            wq, ws = wq_tiles[chunk]
+            z = zp.tile([P, NG, nt, P], F32, name="z")
+            z_tiles[u] = z
+            for tl in range(nt):
+                t = t0 + tl
+                bank = psum.tile([P, NG, P], F32, name="mx", tag="bank")
+                for g in range(2):
+                    cols = slice(g * P, (g + 1) * P)
+                    nc.tensor.matmul_mx(
+                        out=bank[:].rearrange("p g r -> p (g r)"),
+                        lhsT=xq[:, t, cols].bitcast(FP8X4),
+                        lhsT_scale=xs[:, t, cols],
+                        rhs=wq[:, g, :].bitcast(FP8X4),
+                        rhs_scale=ws[:, g, :],
+                        start=(g == 0),
+                        stop=(g == 1),
+                    )
+                nc.vector.tensor_tensor(
+                    out=z[:, :, tl, :],
+                    in0=bank[:],
+                    in1=gsum[:, chunk, :].rearrange("p (g r) -> p g r", g=NG),
+                    op=ALU.add,
+                )
+
         def product(engine, out, in0, in1, op):
-            if engine == 0:
+            if engine == VECTOR:
                 nc.vector.tensor_tensor(out=out, in0=in0, in1=in1, op=op)
             else:
                 nc.gpsimd.tensor_tensor(out=out, in0=in0, in1=in1, op=op)
 
-        def finish(u):
-            k, half = divmod(u, 2)
-            ks = slice(k * P, (k + 1) * P)
+        def sigmoid_gates(u):
+            sig = z_tiles[u][:, 0:3, :, :].rearrange("p g t r -> p (g t r)")
+            nc.scalar.activation(out=sig, in_=sig, func=ACT.Sigmoid)
+
+        def tanh_gate(u):
             z = z_tiles[u]
-            hout = hp.tile([P, NT, P], F32, name="hout")
-            product(0 if u >= NU - TAIL_V else 1, hout[:], z[:, 2], z[:, 1], ALU.mult)
-            t0 = half * NT
-            nc.sync.dma_start(
-                out=out_0[t0:t0 + NT, :, ks].rearrange("t b h -> b t h"), in_=hout[:]
+            nc.scalar.activation(out=z[:, 3], in_=z[:, 3], func=ACT.Tanh)
+
+        def forget(u):
+            chunk, t0, nt = u
+            z = z_tiles[u]
+            c0_view = c0_banks[chunk // 4][:, (chunk % 4) * P:(chunk % 4 + 1) * P]
+            nc.vector.tensor_tensor(
+                out=z[:, 1], in0=z[:, 1],
+                in1=c0_view.unsqueeze(1).to_broadcast([P, nt, P]),
+                op=ALU.mult,
             )
-            if half == 1:
-                nc.sync.dma_start(out=out_1[0, :, ks], in_=hout[:, NT - 1, :])
-                nc.sync.dma_start(out=out_2[0, :, ks], in_=z[:, 3, NT - 1, :])
 
-        c0_banks = {}
+        def update(u, engine):
+            z = z_tiles[u]
+            product(engine, z[:, 0], z[:, 0], z[:, 3], ALU.mult)
 
-        def c0_bank(k):
-            j = k // 4
-            if j not in c0_banks:
-                bank = psum_c0.tile([P, 4 * P], F32, name="c0_bank")
-                nc.tensor.matmul(
-                    bank[:], lhsT=ident_bf[:], rhs=c0_sb[:, 4 * j * P:4 * (j + 1) * P],
-                    start=True, stop=True,
-                )
-                c0_banks[j] = bank
-            return c0_banks[j][:, (k % 4) * P:(k % 4 + 1) * P]
+        def cell(u, engine):
+            z = z_tiles[u]
+            product(engine, z[:, 3], z[:, 0], z[:, 1], ALU.add)
 
-        def elementwise(s):
-            a = s - 1
-            if 0 <= a < NU:
-                z = z_tiles[a]
-                k = a // 2
-                eng = 0 if a >= NU - TAIL_V else 1
-                sig = z[:, 0:3, :, :].rearrange("p g t r -> p (g t r)")
-                nc.scalar.activation(out=sig, in_=sig, func=ACT.Sigmoid)
-                nc.vector.tensor_tensor(
-                    out=z[:, 1], in0=z[:, 1],
-                    in1=c0_bank(k).unsqueeze(1).to_broadcast([P, NT, P]),
-                    op=ALU.mult,
-                )
-                nc.scalar.activation(out=z[:, 3], in_=z[:, 3], func=ACT.Tanh)
-                product(eng, z[:, 0], z[:, 0], z[:, 3], ALU.mult)
-                product(eng, z[:, 3], z[:, 0], z[:, 1], ALU.add)
-            b = s - 2
-            if 0 <= b < NU:
-                z = z_tiles[b]
-                nc.scalar.activation(out=z[:, 1], in_=z[:, 3], func=ACT.Tanh)
-                state["late"] = lambda: finish(b)
+        def tanh_cell(u):
+            z = z_tiles[u]
+            nc.scalar.activation(out=z[:, 1], in_=z[:, 3], func=ACT.Tanh)
 
-        for kind, k in plan:
-            if kind == "h0":
-                bank = transpose_words(h0_raw[:].bitcast(F32))
-                nc.vector.tensor_copy(
-                    out=h_t[:],
-                    in_=bank[:].bitcast(BF16).rearrange("p j (b e) -> p j e b", e=2),
-                )
-            elif kind == "x":
-                banks = [
-                    transpose_for_mx(x_raw[:].bitcast(F32)[:, t, :]) for t in (2 * k, 2 * k + 1)
-                ]
-                for n in range(2):
-                    copy(
-                        COPY_X[n],
-                        xg[:].bitcast(F32)[:, 2 * k + n, :].rearrange(
-                            "p (g r u) -> p g r u", g=2, u=2
-                        ),
-                        regrouped(banks[n]),
-                    )
-                flush_pending()
-                state["pending"].append(lambda pair=k: quantise_x(pair))
-            elif kind == "H":
-                wh_t = whp.tile([P, 4, NG * P], F32, name="wh_t")
-                wh_tiles[k] = wh_t
-                banks = []
-                for g in range(NG):
-                    banks.append(transpose_words(raw_tiles[("H", k, g)][:].bitcast(F32)))
-                    issue_load()
-                for g in range(NG):
-                    copy((1, 0, 1, 0)[g] if k == 0 else COPY_H[g], wh_t[:, :, g * P:(g + 1) * P], banks[g][:])
-                flush_pending()
-                run_late()
-            elif kind == "I":
-                wg = wgp.tile([P, 2, NG, 4 * P], BF16, name="wg", align_bytes=64)
-                wg_tiles[k] = wg
-                banks = []
-                for g in range(NG):
-                    banks.append(transpose_for_mx(raw_tiles[("I", k, g)][:].bitcast(F32)))
-                    issue_load()
-                for g in range(NG):
-                    copy(
-                        (0, 1, 0, 1)[g] if k == 0 else COPY_I[g],
-                        wg[:].bitcast(F32)[:, :, g, :].rearrange("p g (r u) -> p g r u", u=2),
-                        regrouped(banks[g]),
-                    )
-                flush_pending()
-                run_late()
-                state["pending"].append(lambda chunk=k: quantise_w(chunk))
-            elif kind == "hid":
-                wv = wh_tiles[k][:].bitcast(BF16).rearrange("p j (c e) -> p j c e", e=2)
-                bank = psum.tile([P, NG * P], F32, name="hid", tag="bank")
-                for j in range(4):
-                    for e in range(2):
-                        nc.tensor.matmul(
-                            bank[:], lhsT=h_t[:, j, e, :], rhs=wv[:, j, :, e],
-                            start=(j == 0 and e == 0), stop=False,
-                        )
-                nc.tensor.matmul(
-                    bank[:], lhsT=ones[:],
-                    rhs=bias_sb[:, k, :, :].rearrange("p g r -> p (g r)"),
-                    start=False, stop=True,
-                )
-                flush_pending()
-                copy(COPY_G, gsum[:, k, :], bank[:])
-            else:
-                flush_pending()
-                run_late()
-                chunk, half = divmod(k, 2)
-                wq, ws = wq_tiles[chunk]
-                z = zp.tile([P, NG, NT, P], F32, name="z")
-                z_tiles[k] = z
-                for tl in range(NT):
-                    t = half * NT + tl
-                    bank = psum.tile([P, NG, P], F32, name="mx", tag="bank")
-                    for g in range(2):
-                        cols = slice(g * P, (g + 1) * P)
-                        nc.tensor.matmul_mx(
-                            out=bank[:].rearrange("p g r -> p (g r)"),
-                            lhsT=xq[:, t, cols].bitcast(FP8X4),
-                            lhsT_scale=xs[:, t, cols],
-                            rhs=wq[:, g, :].bitcast(FP8X4),
-                            rhs_scale=ws[:, g, :],
-                            start=(g == 0),
-                            stop=(g == 1),
-                        )
-                    nc.vector.tensor_tensor(
-                        out=z[:, :, tl, :],
-                        in0=bank[:],
-                        in1=gsum[:, chunk, :].rearrange("p (g r) -> p g r", g=NG),
-                        op=ALU.add,
-                    )
-                elementwise(k)
-        run_late()
-        for s in range(NU, NU + 2):
-            elementwise(s)
-            run_late()
+        def store(u, engine):
+            chunk, t0, nt = u
+            ks = slice(chunk * P, (chunk + 1) * P)
+            z = z_tiles[u]
+            hout = hp.tile([P, nt, P], F32, name="hout")
+            product(engine, hout[:], z[:, 2], z[:, 1], ALU.mult)
+            if t0 + nt == T:
+                nc.sync.dma_start(out=out_2[0, :, ks], in_=z[:, 3, nt - 1, :])
+            nc.sync.dma_start(
+                out=out_0[t0:t0 + nt, :, ks].rearrange("t b h -> b t h"), in_=hout[:]
+            )
+            if t0 + nt == T:
+                nc.sync.dma_start(out=out_1[0, :, ks], in_=hout[:, nt - 1, :])
+
+        prepare_h0()
+        transpose_hid(0)
+        copy_hid(0, COPY_H_HEAD)
+        matmul_hid(0)
+        for pair in range(4):
+            transpose_x(pair)
+            if pair > 0:
+                quantise_x(pair - 1)
+        transpose_in(0)
+        copy_in(0, COPY_I_HEAD)
+        quantise_x(3)
+        transpose_hid(1)
+        quantise_in(0)
+        copy_hid(1, COPY_H)
+        matmul_hid(1)
+        load_c0_bank(0)
+
+        previous = None
+        for k in range(NCH - 2):
+            first, second = UNITS[2 * k], UNITS[2 * k + 1]
+            matmul_mx(first)
+            if previous is not None:
+                forget(previous)
+                cell(previous, GPSIMD)
+            sigmoid_gates(first)
+            transpose_in(k + 1)
+            copy_in(k + 1, COPY_I)
+            transpose_hid(k + 2)
+            copy_hid(k + 2, COPY_H)
+            if k == 4:
+                load_c0_bank(1)
+            tanh_gate(first)
+            quantise_in(k + 1)
+            forget(first)
+            if previous is not None:
+                tanh_cell(previous)
+                store(previous, GPSIMD)
+            update(first, GPSIMD)
+            cell(first, GPSIMD)
+            matmul_mx(second)
+            sigmoid_gates(second)
+            tanh_gate(second)
+            if k + 2 < NCH - 1:
+                matmul_hid(k + 2)
+            update(second, GPSIMD)
+            tanh_cell(first)
+            store(first, GPSIMD)
+            previous = second
+
+        last = NCH - 1
+        first, second = UNITS[2 * last - 2], UNITS[2 * last - 1]
+        matmul_mx(first)
+        forget(previous)
+        cell(previous, GPSIMD)
+        sigmoid_gates(first)
+        tanh_gate(first)
+        transpose_in(last)
+        copy_in(last, COPY_I)
+        tanh_cell(previous)
+        store(previous, GPSIMD)
+        update(first, GPSIMD)
+        matmul_mx(second)
+        quantise_in(last)
+        forget(first)
+        cell(first, GPSIMD)
+        matmul_hid(last)
+        sigmoid_gates(second)
+        tanh_gate(second)
+        tanh_cell(first)
+        forget(second)
+        update(second, GPSIMD)
+        matmul_mx(TAIL[0])
+        cell(second, GPSIMD)
+        store(first, GPSIMD)
+        sigmoid_gates(TAIL[0])
+        tanh_gate(TAIL[0])
+        matmul_mx(TAIL[1])
+        tanh_cell(second)
+        sigmoid_gates(TAIL[1])
+        tanh_gate(TAIL[1])
+        store(second, GPSIMD)
+        forget(TAIL[0])
+        matmul_mx(TAIL[2])
+        update(TAIL[0], VECTOR)
+        cell(TAIL[0], VECTOR)
+        sigmoid_gates(TAIL[2])
+        tanh_gate(TAIL[2])
+        tanh_cell(TAIL[0])
+        forget(TAIL[1])
+        matmul_mx(TAIL[3])
+        update(TAIL[1], VECTOR)
+        sigmoid_gates(TAIL[3])
+        tanh_gate(TAIL[3])
+        cell(TAIL[1], VECTOR)
+        store(TAIL[0], VECTOR)
+        tanh_cell(TAIL[1])
+        forget(TAIL[2])
+        update(TAIL[2], VECTOR)
+        forget(TAIL[3])
+        cell(TAIL[2], VECTOR)
+        update(TAIL[3], VECTOR)
+        tanh_cell(TAIL[2])
+        store(TAIL[1], VECTOR)
+        cell(TAIL[3], VECTOR)
+        store(TAIL[2], VECTOR)
+        tanh_cell(TAIL[3])
+        store(TAIL[3], VECTOR)

@@ -16,10 +16,10 @@ P = 128
 B, T, I, H = 128, 8, 1024, 1024
 NG = 4
 NCH = H // P
-RAW_BUFS = 24
+RAW_BUFS = 12
 VECTOR, SCALAR, GPSIMD = 0, 1, 2
 COPY_X = (VECTOR, SCALAR)
-COPY_I = (VECTOR, VECTOR, VECTOR, VECTOR)
+COPY_I = (SCALAR, SCALAR, SCALAR, SCALAR)
 COPY_I_HEAD = (VECTOR, SCALAR, VECTOR, SCALAR)
 COPY_H = (SCALAR, SCALAR, SCALAR, SCALAR)
 COPY_H_HEAD = (SCALAR, VECTOR, SCALAR, VECTOR)
@@ -48,10 +48,11 @@ def tile_naivelstm_pa_kernel(
         ctx.enter_context(tc.manual_schedule())
         const = ctx.enter_context(tc.tile_pool(name="const", bufs=1))
         raw = ctx.enter_context(tc.tile_pool(name="raw", bufs=RAW_BUFS))
+        rawq = ctx.enter_context(tc.tile_pool(name="rawq", bufs=2))
         wgp = ctx.enter_context(tc.tile_pool(name="wgp", bufs=2))
         wqp = ctx.enter_context(tc.tile_pool(name="wqp", bufs=3))
         whp = ctx.enter_context(tc.tile_pool(name="whp", bufs=2))
-        zp = ctx.enter_context(tc.tile_pool(name="zp", bufs=5))
+        zp = ctx.enter_context(tc.tile_pool(name="zp", bufs=6))
         hp = ctx.enter_context(tc.tile_pool(name="hp", bufs=3))
         psum = ctx.enter_context(tc.psum_pool(name="psum", bufs=7))
         psum_c0 = ctx.enter_context(tc.psum_pool(name="psum_c0", bufs=1))
@@ -64,6 +65,8 @@ def tile_naivelstm_pa_kernel(
         h0_raw = const.tile([P, H], BF16, name="h0_raw")
         c0_sb = const.tile([P, H], BF16, name="c0_sb")
         h_t = const.tile([P, 4, 2, P], BF16, name="h_t")
+        h0_perm = const.tile([P, H], BF16, name="h0_perm")
+        h_tq = const.tile([P, 4, 2, P], BF16, name="h_tq")
         x_raw = const.tile([P, T, I], BF16, name="x_raw")
         xg = const.tile([P, T, I], BF16, name="xg", align_bytes=64)
         xq = const.tile([P, T, I // 4], U32, name="xq", align_bytes=64)
@@ -75,25 +78,33 @@ def tile_naivelstm_pa_kernel(
         nc.vector.memset(scratch[:], 0.0)
         nc.vector.memset(ones[:], 1.0)
 
-        load_order = [("H", 0), ("x", 0), ("x", 1), ("x", 2), ("x", 3), ("I", 0), ("H", 1)]
-        for k in range(NCH):
-            if k + 1 < NCH:
-                load_order.append(("I", k + 1))
-            if k + 2 < NCH:
-                load_order.append(("H", k + 2))
-        weights = [(kind, k, g) for kind, k in load_order if kind != "x" for g in range(NG)]
         raw_tiles = {}
+        in_order = [("H", 0), ("I", 0), ("H", 1)] + [("I", k) for k in range(1, NCH)]
+        whole = [(kind, k, g) for kind, k in in_order for g in range(NG)]
         cursor = [0]
 
-        def issue_load():
+        def load_rows():
             n = cursor[0]
-            if n < len(weights):
-                kind, k, g = weights[n]
+            if n < len(whole):
+                kind, k, g = whole[n]
                 w = w_hid[g] if kind == "H" else w_in[g]
                 wraw = raw.tile([P, I], BF16, name="wraw", tag="wraw")
                 nc.sync.dma_start(out=wraw[:], in_=w[k * P:(k + 1) * P, :])
-                raw_tiles[weights[n]] = wraw
+                raw_tiles[whole[n]] = wraw
                 cursor[0] = n + 1
+
+        def load_quadrants(k):
+            if k < NCH:
+                wraw = rawq.tile([P, NG, 4, 256], BF16, name="wrawq", align_bytes=64)
+                for g in range(NG):
+                    for q in (0, 2, 1, 3):
+                        nc.sync.dma_start(
+                            out=wraw[32 * q:32 * (q + 1), g, :, :],
+                            in_=w_hid[g][k * P:(k + 1) * P, 256 * q:256 * (q + 1)].rearrange(
+                                "(m r) e -> r m e", r=32
+                            ),
+                        )
+                raw_tiles[("Q", k)] = wraw
 
         nc.sync.dma_start(out=h0_raw[:], in_=h0[0])
         for g in range(NG):
@@ -108,14 +119,15 @@ def tile_naivelstm_pa_kernel(
         nc.scalar.activation(out=scratch[:], in_=scratch[:], func=ACT.Sigmoid)
         nc.gpsimd.dma_start(out=c0_sb[:], in_=c0[0])
         make_identity(nc, ident_bf[:])
-        for kind, k in load_order:
-            if kind == "x":
-                nc.sync.dma_start(
-                    out=x_raw[:, 2 * k:2 * k + 2, :], in_=inputs[:, 2 * k:2 * k + 2, :]
-                )
-            elif cursor[0] < RAW_BUFS:
-                for g in range(NG):
-                    issue_load()
+        for g in range(NG):
+            load_rows()
+        for pair in range(4):
+            nc.sync.dma_start(
+                out=x_raw[:, 2 * pair:2 * pair + 2, :], in_=inputs[:, 2 * pair:2 * pair + 2, :]
+            )
+        for n in range(2 * NG):
+            load_rows()
+        load_quadrants(2)
 
         def copy(engine, out, in_):
             if engine == VECTOR:
@@ -174,26 +186,53 @@ def tile_naivelstm_pa_kernel(
                 in_=xg[:, tt, :].rearrange("p t c -> p (t c)"),
             )
 
+        def prepare_h0_quadrants():
+            nc.vector.tensor_copy(
+                out=h0_perm[:].rearrange("p (j q c) -> p j q c", j=4, q=4),
+                in_=h0_raw[:].rearrange("p (q j c) -> p j q c", j=4, q=4),
+            )
+            bank = transpose_words(h0_perm[:].bitcast(F32))
+            nc.vector.tensor_copy(
+                out=h_tq[:],
+                in_=bank[:].bitcast(BF16).rearrange("p j (b e) -> p j e b", e=2),
+            )
+
+        def transpose_quadrants(k):
+            wh_t = whp.tile([P, 4, NG * P], F32, name="wh_t", align_bytes=64)
+            wh_tiles[k] = wh_t
+            nc.vector.transpose(
+                out=wh_t[:].rearrange("p g c -> p (g c)"),
+                in_=raw_tiles[("Q", k)][:].rearrange("p g m e -> p (g m e)").bitcast(F32),
+            )
+            load_quadrants(k + 2)
+
         def transpose_hid(k):
             banks = []
             for g in range(NG):
                 banks.append(transpose_words(raw_tiles[("H", k, g)][:].bitcast(F32)))
-                issue_load()
+                load_rows()
             banks_of["H"] = banks
 
         def copy_hid(k, engines):
-            wh_t = whp.tile([P, 4, NG * P], F32, name="wh_t")
+            wh_t = whp.tile([P, 4, NG * P], F32, name="wh_t", align_bytes=64)
             wh_tiles[k] = wh_t
             for g in range(NG):
                 copy(engines[g], wh_t[:, :, g * P:(g + 1) * P], banks_of["H"][g][:])
 
         def matmul_hid(k):
-            wv = wh_tiles[k][:].bitcast(BF16).rearrange("p j (c e) -> p j c e", e=2)
             bank = psum.tile([P, NG * P], F32, name="hid", tag="bank")
+            if k < 2:
+                wv = wh_tiles[k][:].bitcast(BF16).rearrange("p j (c e) -> p j e c", e=2)
+                out, ht = bank[:], h_t
+            else:
+                wv = wh_tiles[k][:].bitcast(BF16).rearrange(
+                    "p g (m j r e) -> p j e (g m) r", m=4, j=4, e=2
+                )
+                out, ht = bank[:].rearrange("p (m r) -> p m r", r=32), h_tq
             for j in range(4):
                 for e in range(2):
                     nc.tensor.matmul(
-                        bank[:], lhsT=h_t[:, j, e, :], rhs=wv[:, j, :, e],
+                        out, lhsT=ht[:, j, e, :], rhs=wv[:, j, e],
                         start=(j == 0 and e == 0), stop=False,
                     )
             nc.tensor.matmul(
@@ -207,7 +246,7 @@ def tile_naivelstm_pa_kernel(
             banks = []
             for g in range(NG):
                 banks.append(transpose_for_mx(raw_tiles[("I", k, g)][:].bitcast(F32)))
-                issue_load()
+                load_rows()
             banks_of["I"] = banks
 
         def copy_in(k, engines):
@@ -316,6 +355,7 @@ def tile_naivelstm_pa_kernel(
 
         prepare_h0()
         transpose_hid(0)
+        load_quadrants(3)
         copy_hid(0, COPY_H_HEAD)
         matmul_hid(0)
         for pair in range(4):
@@ -330,6 +370,7 @@ def tile_naivelstm_pa_kernel(
         copy_hid(1, COPY_H)
         matmul_hid(1)
         load_c0_bank(0)
+        prepare_h0_quadrants()
 
         previous = None
         for k in range(NCH - 2):
@@ -338,22 +379,21 @@ def tile_naivelstm_pa_kernel(
             if previous is not None:
                 forget(previous)
                 cell(previous, GPSIMD)
-            sigmoid_gates(first)
+            transpose_quadrants(k + 2)
             transpose_in(k + 1)
             copy_in(k + 1, COPY_I)
-            transpose_hid(k + 2)
-            copy_hid(k + 2, COPY_H)
+            sigmoid_gates(first)
             if k == 4:
                 load_c0_bank(1)
             tanh_gate(first)
-            quantise_in(k + 1)
-            forget(first)
             if previous is not None:
                 tanh_cell(previous)
                 store(previous, GPSIMD)
             update(first, GPSIMD)
-            cell(first, GPSIMD)
             matmul_mx(second)
+            quantise_in(k + 1)
+            forget(first)
+            cell(first, GPSIMD)
             sigmoid_gates(second)
             tanh_gate(second)
             if k + 2 < NCH - 1:

@@ -119,15 +119,20 @@ def tile_naivelstm_pa_kernel(
         nc.scalar.activation(out=scratch[:], in_=scratch[:], func=ACT.Sigmoid)
         nc.gpsimd.dma_start(out=c0_sb[:], in_=c0[0])
         make_identity(nc, ident_bf[:])
+        def load_x(pair):
+            tt = slice(2 * pair, 2 * pair + 2)
+            nc.sync.dma_start(out=x_raw[:, tt, :], in_=inputs[:, tt, :])
+
         for g in range(NG):
             load_rows()
-        for pair in range(4):
-            nc.sync.dma_start(
-                out=x_raw[:, 2 * pair:2 * pair + 2, :], in_=inputs[:, 2 * pair:2 * pair + 2, :]
-            )
-        for n in range(2 * NG):
+        load_x(0)
+        load_x(1)
+        for g in range(NG):
             load_rows()
-        load_quadrants(2)
+        load_x(2)
+        load_x(3)
+        for g in range(NG):
+            load_rows()
 
         def copy(engine, out, in_):
             if engine == VECTOR:
@@ -197,14 +202,16 @@ def tile_naivelstm_pa_kernel(
                 in_=bank[:].bitcast(BF16).rearrange("p j (b e) -> p j e b", e=2),
             )
 
-        def transpose_quadrants(k):
-            wh_t = whp.tile([P, 4, NG * P], F32, name="wh_t", align_bytes=64)
-            wh_tiles[k] = wh_t
+        def transpose_quadrants(k, part):
+            if part == 0:
+                wh_tiles[k] = whp.tile([P, 4, NG * P], F32, name="wh_t", align_bytes=64)
+            gg = slice(2 * part, 2 * part + 2)
             nc.vector.transpose(
-                out=wh_t[:].rearrange("p g c -> p (g c)"),
-                in_=raw_tiles[("Q", k)][:].rearrange("p g m e -> p (g m e)").bitcast(F32),
+                out=wh_tiles[k][:, gg, :].rearrange("p g c -> p (g c)"),
+                in_=raw_tiles[("Q", k)][:, gg, :, :].rearrange("p g m e -> p (g m e)").bitcast(F32),
             )
-            load_quadrants(k + 2)
+            if part == 1:
+                load_quadrants(k + 2)
 
         def transpose_hid(k):
             banks = []
@@ -355,52 +362,60 @@ def tile_naivelstm_pa_kernel(
 
         prepare_h0()
         transpose_hid(0)
-        load_quadrants(3)
+        load_quadrants(2)
         copy_hid(0, COPY_H_HEAD)
-        matmul_hid(0)
-        for pair in range(4):
-            transpose_x(pair)
-            if pair > 0:
-                quantise_x(pair - 1)
+        transpose_x(0)
+        transpose_x(1)
+        quantise_x(0)
         transpose_in(0)
+        load_quadrants(3)
         copy_in(0, COPY_I_HEAD)
-        quantise_x(3)
-        transpose_hid(1)
+        quantise_x(1)
+        matmul_hid(0)
         quantise_in(0)
-        copy_hid(1, COPY_H)
-        matmul_hid(1)
-        load_c0_bank(0)
         prepare_h0_quadrants()
 
+        older = None
         previous = None
         for k in range(NCH - 2):
             first, second = UNITS[2 * k], UNITS[2 * k + 1]
             matmul_mx(first)
-            if previous is not None:
+            if k == 0:
+                transpose_x(2)
+                transpose_x(3)
+                load_c0_bank(0)
+                quantise_x(2)
+                transpose_hid(1)
+                copy_hid(1, COPY_H)
+                quantise_x(3)
+            else:
                 forget(previous)
                 cell(previous, GPSIMD)
-            transpose_quadrants(k + 2)
             transpose_in(k + 1)
             copy_in(k + 1, COPY_I)
+            transpose_quadrants(k + 2, 0)
+            transpose_quadrants(k + 2, 1)
+            quantise_in(k + 1)
+            if k > 0:
+                tanh_cell(older)
+                store(older, GPSIMD)
             sigmoid_gates(first)
+            tanh_gate(first)
             if k == 4:
                 load_c0_bank(1)
-            tanh_gate(first)
-            if previous is not None:
+            matmul_hid(k + 1)
+            if k > 0:
                 tanh_cell(previous)
-                store(previous, GPSIMD)
-            update(first, GPSIMD)
-            matmul_mx(second)
-            quantise_in(k + 1)
             forget(first)
+            update(first, GPSIMD)
+            if k > 0:
+                store(previous, GPSIMD)
             cell(first, GPSIMD)
+            matmul_mx(second)
             sigmoid_gates(second)
             tanh_gate(second)
-            if k + 2 < NCH - 1:
-                matmul_hid(k + 2)
             update(second, GPSIMD)
-            tanh_cell(first)
-            store(first, GPSIMD)
+            older = first
             previous = second
 
         last = NCH - 1
@@ -408,28 +423,30 @@ def tile_naivelstm_pa_kernel(
         matmul_mx(first)
         forget(previous)
         cell(previous, GPSIMD)
+        matmul_mx(second)
+        transpose_in(last)
+        copy_in(last, (VECTOR, VECTOR, VECTOR, VECTOR))
         sigmoid_gates(first)
         tanh_gate(first)
-        transpose_in(last)
-        copy_in(last, COPY_I)
-        tanh_cell(previous)
-        store(previous, GPSIMD)
-        update(first, GPSIMD)
-        matmul_mx(second)
         quantise_in(last)
-        forget(first)
-        cell(first, GPSIMD)
+        tanh_cell(older)
+        store(older, GPSIMD)
         matmul_hid(last)
+        forget(first)
+        update(first, GPSIMD)
+        cell(first, GPSIMD)
         sigmoid_gates(second)
         tanh_gate(second)
-        tanh_cell(first)
+        tanh_cell(previous)
+        store(previous, GPSIMD)
         forget(second)
         update(second, GPSIMD)
         matmul_mx(TAIL[0])
         cell(second, GPSIMD)
-        store(first, GPSIMD)
+        tanh_cell(first)
         sigmoid_gates(TAIL[0])
         tanh_gate(TAIL[0])
+        store(first, GPSIMD)
         matmul_mx(TAIL[1])
         tanh_cell(second)
         sigmoid_gates(TAIL[1])

@@ -53,7 +53,7 @@ def tile_naivelstm_pa_kernel(
         wqp = ctx.enter_context(tc.tile_pool(name="wqp", bufs=3))
         whp = ctx.enter_context(tc.tile_pool(name="whp", bufs=2))
         zp = ctx.enter_context(tc.tile_pool(name="zp", bufs=6))
-        hp = ctx.enter_context(tc.tile_pool(name="hp", bufs=3))
+        hp = ctx.enter_context(tc.tile_pool(name="hp", bufs=6))
         psum = ctx.enter_context(tc.psum_pool(name="psum", bufs=7))
         psum_c0 = ctx.enter_context(tc.psum_pool(name="psum_c0", bufs=1))
 
@@ -324,9 +324,16 @@ def tile_naivelstm_pa_kernel(
             z = z_tiles[u]
             nc.scalar.activation(out=z[:, 3], in_=z[:, 3], func=ACT.Tanh)
 
-        def forget(u):
+        def forget(u, engine=VECTOR):
             chunk, t0, nt = u
             z = z_tiles[u]
+            if engine == GPSIMD:
+                nc.gpsimd.tensor_tensor(
+                    out=z[:, 1], in0=z[:, 1],
+                    in1=c0_sb[:, chunk * P:(chunk + 1) * P].unsqueeze(1).to_broadcast([P, nt, P]),
+                    op=ALU.mult,
+                )
+                return
             c0_view = c0_banks[chunk // 4][:, (chunk % 4) * P:(chunk % 4 + 1) * P]
             nc.vector.tensor_tensor(
                 out=z[:, 1], in0=z[:, 1],
@@ -406,7 +413,7 @@ def tile_naivelstm_pa_kernel(
             matmul_hid(k + 1)
             if k > 0:
                 tanh_cell(previous)
-            forget(first)
+            forget(first, GPSIMD)
             update(first, GPSIMD)
             if k > 0:
                 store(previous, GPSIMD)
@@ -422,59 +429,59 @@ def tile_naivelstm_pa_kernel(
         first, second = UNITS[2 * last - 2], UNITS[2 * last - 1]
         matmul_mx(first)
         forget(previous)
-        cell(previous, GPSIMD)
         matmul_mx(second)
         transpose_in(last)
-        copy_in(last, (VECTOR, VECTOR, VECTOR, VECTOR))
         sigmoid_gates(first)
+        copy_in(last, (SCALAR, SCALAR, SCALAR, SCALAR))
         tanh_gate(first)
-        quantise_in(last)
-        tanh_cell(older)
-        store(older, GPSIMD)
-        matmul_hid(last)
         forget(first)
-        update(first, GPSIMD)
-        cell(first, GPSIMD)
+        quantise_in(last)
         sigmoid_gates(second)
         tanh_gate(second)
+        matmul_hid(last)
+        cell(previous, VECTOR)
+        update(first, VECTOR)
+        cell(first, VECTOR)
+        tanh_cell(older)
+        forget(second)
+        update(second, VECTOR)
+        store(older, GPSIMD)
+        matmul_mx(TAIL[0])
+        cell(second, VECTOR)
         tanh_cell(previous)
         store(previous, GPSIMD)
-        forget(second)
-        update(second, GPSIMD)
-        matmul_mx(TAIL[0])
-        cell(second, GPSIMD)
-        tanh_cell(first)
         sigmoid_gates(TAIL[0])
         tanh_gate(TAIL[0])
-        store(first, GPSIMD)
         matmul_mx(TAIL[1])
-        tanh_cell(second)
+        tanh_cell(first)
+        store(first, GPSIMD)
         sigmoid_gates(TAIL[1])
         tanh_gate(TAIL[1])
-        store(second, GPSIMD)
-        forget(TAIL[0])
         matmul_mx(TAIL[2])
+        tanh_cell(second)
+        forget(TAIL[0])
         update(TAIL[0], VECTOR)
         cell(TAIL[0], VECTOR)
         sigmoid_gates(TAIL[2])
         tanh_gate(TAIL[2])
-        tanh_cell(TAIL[0])
-        forget(TAIL[1])
         matmul_mx(TAIL[3])
-        update(TAIL[1], VECTOR)
+        store(second, GPSIMD)
+        tanh_cell(TAIL[0])
         sigmoid_gates(TAIL[3])
         tanh_gate(TAIL[3])
+        forget(TAIL[1])
+        update(TAIL[1], VECTOR)
         cell(TAIL[1], VECTOR)
-        store(TAIL[0], VECTOR)
-        tanh_cell(TAIL[1])
         forget(TAIL[2])
         update(TAIL[2], VECTOR)
-        forget(TAIL[3])
         cell(TAIL[2], VECTOR)
-        update(TAIL[3], VECTOR)
+        tanh_cell(TAIL[1])
+        store(TAIL[0], VECTOR)
         tanh_cell(TAIL[2])
-        store(TAIL[1], VECTOR)
+        forget(TAIL[3])
+        update(TAIL[3], VECTOR)
         cell(TAIL[3], VECTOR)
-        store(TAIL[2], VECTOR)
+        store(TAIL[1], VECTOR)
         tanh_cell(TAIL[3])
+        store(TAIL[2], VECTOR)
         store(TAIL[3], VECTOR)

@@ -324,16 +324,9 @@ def tile_naivelstm_pa_kernel(
             z = z_tiles[u]
             nc.scalar.activation(out=z[:, 3], in_=z[:, 3], func=ACT.Tanh)
 
-        def forget(u, engine=VECTOR):
+        def forget(u):
             chunk, t0, nt = u
             z = z_tiles[u]
-            if engine == GPSIMD:
-                nc.gpsimd.tensor_tensor(
-                    out=z[:, 1], in0=z[:, 1],
-                    in1=c0_sb[:, chunk * P:(chunk + 1) * P].unsqueeze(1).to_broadcast([P, nt, P]),
-                    op=ALU.mult,
-                )
-                return
             c0_view = c0_banks[chunk // 4][:, (chunk % 4) * P:(chunk % 4 + 1) * P]
             nc.vector.tensor_tensor(
                 out=z[:, 1], in0=z[:, 1],
@@ -408,17 +401,17 @@ def tile_naivelstm_pa_kernel(
                 store(older, GPSIMD)
             sigmoid_gates(first)
             tanh_gate(first)
+            matmul_hid(k + 1)
             if k == 4:
                 load_c0_bank(1)
-            matmul_hid(k + 1)
             if k > 0:
                 tanh_cell(previous)
-            forget(first, GPSIMD)
             update(first, GPSIMD)
             if k > 0:
                 store(previous, GPSIMD)
-            cell(first, GPSIMD)
             matmul_mx(second)
+            forget(first)
+            cell(first, GPSIMD)
             sigmoid_gates(second)
             tanh_gate(second)
             update(second, GPSIMD)
@@ -435,11 +428,11 @@ def tile_naivelstm_pa_kernel(
         copy_in(last, (SCALAR, SCALAR, SCALAR, SCALAR))
         tanh_gate(first)
         forget(first)
+        cell(previous, VECTOR)
         quantise_in(last)
         sigmoid_gates(second)
         tanh_gate(second)
         matmul_hid(last)
-        cell(previous, VECTOR)
         update(first, VECTOR)
         cell(first, VECTOR)
         tanh_cell(older)

@@ -434,9 +434,9 @@ def tile_naivelstm_pa_kernel(
         tanh_gate(second)
         matmul_hid(last)
         update(first, VECTOR)
+        forget(second)
         cell(first, VECTOR)
         tanh_cell(older)
-        forget(second)
         update(second, VECTOR)
         store(older, GPSIMD)
         matmul_mx(TAIL[0])
@@ -452,28 +452,28 @@ def tile_naivelstm_pa_kernel(
         tanh_gate(TAIL[1])
         matmul_mx(TAIL[2])
         tanh_cell(second)
-        forget(TAIL[0])
-        update(TAIL[0], VECTOR)
-        cell(TAIL[0], VECTOR)
         sigmoid_gates(TAIL[2])
         tanh_gate(TAIL[2])
         matmul_mx(TAIL[3])
         store(second, GPSIMD)
-        tanh_cell(TAIL[0])
+        forget(TAIL[0])
+        forget(TAIL[1])
+        update(TAIL[0], VECTOR)
+        update(TAIL[1], VECTOR)
+        cell(TAIL[0], VECTOR)
+        cell(TAIL[1], VECTOR)
         sigmoid_gates(TAIL[3])
         tanh_gate(TAIL[3])
-        forget(TAIL[1])
-        update(TAIL[1], VECTOR)
-        cell(TAIL[1], VECTOR)
         forget(TAIL[2])
-        update(TAIL[2], VECTOR)
-        cell(TAIL[2], VECTOR)
+        tanh_cell(TAIL[0])
         tanh_cell(TAIL[1])
-        store(TAIL[0], VECTOR)
-        tanh_cell(TAIL[2])
+        update(TAIL[2], VECTOR)
         forget(TAIL[3])
+        cell(TAIL[2], VECTOR)
         update(TAIL[3], VECTOR)
+        store(TAIL[0], VECTOR)
         cell(TAIL[3], VECTOR)
+        tanh_cell(TAIL[2])
         store(TAIL[1], VECTOR)
         tanh_cell(TAIL[3])
         store(TAIL[2], VECTOR)

@@ -18,7 +18,8 @@ NG = 4
 NCH = H // P
 RAW_BUFS = 12
 VECTOR, SCALAR, GPSIMD = 0, 1, 2
-COPY_X = (VECTOR, SCALAR)
+COPY_X_HEAD = (VECTOR, SCALAR)
+COPY_X = (VECTOR, VECTOR)
 COPY_I = (SCALAR, SCALAR, SCALAR, SCALAR)
 COPY_I_HEAD = (VECTOR, SCALAR, VECTOR, SCALAR)
 COPY_H = (SCALAR, SCALAR, SCALAR, SCALAR)
@@ -53,6 +54,7 @@ def tile_naivelstm_pa_kernel(
         wqp = ctx.enter_context(tc.tile_pool(name="wqp", bufs=3))
         whp = ctx.enter_context(tc.tile_pool(name="whp", bufs=2))
         zp = ctx.enter_context(tc.tile_pool(name="zp", bufs=6))
+        perm = ctx.enter_context(tc.tile_pool(name="perm", bufs=4))
         hp = ctx.enter_context(tc.tile_pool(name="hp", bufs=6))
         psum = ctx.enter_context(tc.psum_pool(name="psum", bufs=7))
         psum_c0 = ctx.enter_context(tc.psum_pool(name="psum_c0", bufs=1))
@@ -155,9 +157,18 @@ def tile_naivelstm_pa_kernel(
                     )
             return bank
 
+        def permuted(words):
+            tile = perm.tile([P, I // 2], F32, name="perm")
+            nc.vector.tensor_copy(
+                out=tile[:].rearrange("p (g u w) -> p g u w", g=2, u=2),
+                in_=words.rearrange("p (g w u) -> p g u w", g=2, u=2),
+            )
+            return tile[:]
+
         def regrouped(bank):
             return bank[:].rearrange("p (g u) r -> p g r u", u=2)
 
+        permuted_tiles = {}
         wh_tiles = {}
         wg_tiles = {}
         wq_tiles = {}
@@ -172,11 +183,23 @@ def tile_naivelstm_pa_kernel(
                 in_=bank[:].bitcast(BF16).rearrange("p j (b e) -> p j e b", e=2),
             )
 
-        def transpose_x(pair):
+        def permute_x(pair):
+            for t in (2 * pair, 2 * pair + 1):
+                permuted_tiles[("x", t)] = permuted(x_raw[:].bitcast(F32)[:, t, :])
+
+        def permute_in(k):
+            for g in range(NG):
+                permuted_tiles[(k, g)] = permuted(raw_tiles[("I", k, g)][:].bitcast(F32))
+
+        def transpose_x(pair, engines):
             for n in range(2):
-                bank = transpose_for_mx(x_raw[:].bitcast(F32)[:, 2 * pair + n, :])
+                t = 2 * pair + n
+                if ("x", t) in permuted_tiles:
+                    bank = transpose_words(permuted_tiles[("x", t)])
+                else:
+                    bank = transpose_for_mx(x_raw[:].bitcast(F32)[:, t, :])
                 copy(
-                    COPY_X[n],
+                    engines[n],
                     xg[:].bitcast(F32)[:, 2 * pair + n, :].rearrange(
                         "p (g r u) -> p g r u", g=2, u=2
                     ),
@@ -197,7 +220,7 @@ def tile_naivelstm_pa_kernel(
                 in_=h0_raw[:].rearrange("p (q j c) -> p j q c", j=4, q=4),
             )
             bank = transpose_words(h0_perm[:].bitcast(F32))
-            nc.vector.tensor_copy(
+            nc.scalar.copy(
                 out=h_tq[:],
                 in_=bank[:].bitcast(BF16).rearrange("p j (b e) -> p j e b", e=2),
             )
@@ -252,7 +275,10 @@ def tile_naivelstm_pa_kernel(
         def transpose_in(k):
             banks = []
             for g in range(NG):
-                banks.append(transpose_for_mx(raw_tiles[("I", k, g)][:].bitcast(F32)))
+                if (k, g) in permuted_tiles:
+                    banks.append(transpose_words(permuted_tiles[(k, g)]))
+                else:
+                    banks.append(transpose_for_mx(raw_tiles[("I", k, g)][:].bitcast(F32)))
                 load_rows()
             banks_of["I"] = banks
 
@@ -361,11 +387,12 @@ def tile_naivelstm_pa_kernel(
                 nc.sync.dma_start(out=out_1[0, :, ks], in_=hout[:, nt - 1, :])
 
         prepare_h0()
+        prepare_h0_quadrants()
         transpose_hid(0)
         load_quadrants(2)
         copy_hid(0, COPY_H_HEAD)
-        transpose_x(0)
-        transpose_x(1)
+        transpose_x(0, COPY_X_HEAD)
+        transpose_x(1, COPY_X_HEAD)
         quantise_x(0)
         transpose_in(0)
         load_quadrants(3)
@@ -373,42 +400,55 @@ def tile_naivelstm_pa_kernel(
         quantise_x(1)
         matmul_hid(0)
         quantise_in(0)
-        prepare_h0_quadrants()
+        permute_x(2)
+        permute_x(3)
 
-        older = None
-        previous = None
-        for k in range(NCH - 2):
+        older, previous = UNITS[0], UNITS[1]
+        matmul_mx(older)
+        transpose_x(2, COPY_X_HEAD)
+        transpose_x(3, COPY_X_HEAD)
+        load_c0_bank(0)
+        permute_in(1)
+        quantise_x(2)
+        transpose_hid(1)
+        copy_hid(1, COPY_H)
+        quantise_x(3)
+        transpose_in(1)
+        copy_in(1, COPY_I)
+        transpose_quadrants(2, 0)
+        quantise_in(1)
+        sigmoid_gates(older)
+        tanh_gate(older)
+        matmul_hid(1)
+        update(older, GPSIMD)
+        matmul_mx(previous)
+        transpose_quadrants(2, 1)
+        forget(older)
+        cell(older, GPSIMD)
+        sigmoid_gates(previous)
+        tanh_gate(previous)
+        update(previous, GPSIMD)
+
+        for k in range(1, NCH - 2):
             first, second = UNITS[2 * k], UNITS[2 * k + 1]
             matmul_mx(first)
-            if k == 0:
-                transpose_x(2)
-                transpose_x(3)
-                load_c0_bank(0)
-                quantise_x(2)
-                transpose_hid(1)
-                copy_hid(1, COPY_H)
-                quantise_x(3)
-            else:
-                forget(previous)
-                cell(previous, GPSIMD)
+            forget(previous)
+            cell(previous, GPSIMD)
             transpose_in(k + 1)
             copy_in(k + 1, COPY_I)
             transpose_quadrants(k + 2, 0)
             transpose_quadrants(k + 2, 1)
             quantise_in(k + 1)
-            if k > 0:
-                tanh_cell(older)
-                store(older, GPSIMD)
+            tanh_cell(older)
+            store(older, GPSIMD)
             sigmoid_gates(first)
             tanh_gate(first)
             matmul_hid(k + 1)
             if k == 4:
                 load_c0_bank(1)
-            if k > 0:
-                tanh_cell(previous)
+            tanh_cell(previous)
             update(first, GPSIMD)
-            if k > 0:
-                store(previous, GPSIMD)
+            store(previous, GPSIMD)
             matmul_mx(second)
             forget(first)
             cell(first, GPSIMD)

@@ -169,6 +169,7 @@ def tile_naivelstm_pa_kernel(
             return bank[:].rearrange("p (g u) r -> p g r u", u=2)
 
         permuted_tiles = {}
+        in_banks = {}
         wh_tiles = {}
         wg_tiles = {}
         wq_tiles = {}
@@ -190,6 +191,16 @@ def tile_naivelstm_pa_kernel(
         def permute_in(k):
             for g in range(NG):
                 permuted_tiles[(k, g)] = permuted(raw_tiles[("I", k, g)][:].bitcast(F32))
+
+        def permute_some(k, gates, engine):
+            for g in gates:
+                tile = perm.tile([P, I // 2], F32, name="perm")
+                copy(
+                    engine,
+                    tile[:].rearrange("p (g u w) -> p g u w", g=2, u=2),
+                    raw_tiles[("I", k, g)][:].bitcast(F32).rearrange("p (g w u) -> p g u w", g=2, u=2),
+                )
+                permuted_tiles[(k, g)] = tile[:]
 
         def transpose_x(pair, engines):
             for n in range(2):
@@ -272,24 +283,23 @@ def tile_naivelstm_pa_kernel(
             )
             nc.scalar.copy(out=gsum[:, k, :], in_=bank[:])
 
-        def transpose_in(k):
-            banks = []
-            for g in range(NG):
+        def transpose_in(k, gates=range(NG)):
+            for g in gates:
                 if (k, g) in permuted_tiles:
-                    banks.append(transpose_words(permuted_tiles[(k, g)]))
+                    bank = transpose_words(permuted_tiles[(k, g)])
                 else:
-                    banks.append(transpose_for_mx(raw_tiles[("I", k, g)][:].bitcast(F32)))
+                    bank = transpose_for_mx(raw_tiles[("I", k, g)][:].bitcast(F32))
+                in_banks[(k, g)] = bank
                 load_rows()
-            banks_of["I"] = banks
 
-        def copy_in(k, engines):
-            wg = wgp.tile([P, 2, NG, 4 * P], BF16, name="wg", align_bytes=64)
-            wg_tiles[k] = wg
-            for g in range(NG):
+        def copy_in(k, engines, gates=range(NG)):
+            if k not in wg_tiles:
+                wg_tiles[k] = wgp.tile([P, 2, NG, 4 * P], BF16, name="wg", align_bytes=64)
+            for g in gates:
                 copy(
                     engines[g],
-                    wg[:].bitcast(F32)[:, :, g, :].rearrange("p g (r u) -> p g r u", u=2),
-                    regrouped(banks_of["I"][g]),
+                    wg_tiles[k][:].bitcast(F32)[:, :, g, :].rearrange("p g (r u) -> p g r u", u=2),
+                    regrouped(in_banks[(k, g)]),
                 )
 
         def quantise_in(k):
@@ -407,7 +417,6 @@ def tile_naivelstm_pa_kernel(
         matmul_mx(older)
         transpose_x(2, COPY_X_HEAD)
         transpose_x(3, COPY_X_HEAD)
-        load_c0_bank(0)
         permute_in(1)
         quantise_x(2)
         transpose_hid(1)
@@ -419,10 +428,11 @@ def tile_naivelstm_pa_kernel(
         quantise_in(1)
         sigmoid_gates(older)
         tanh_gate(older)
+        matmul_mx(previous)
         matmul_hid(1)
         update(older, GPSIMD)
-        matmul_mx(previous)
         transpose_quadrants(2, 1)
+        load_c0_bank(0)
         forget(older)
         cell(older, GPSIMD)
         sigmoid_gates(previous)
@@ -449,6 +459,8 @@ def tile_naivelstm_pa_kernel(
             tanh_cell(previous)
             update(first, GPSIMD)
             store(previous, GPSIMD)
+            if k < NCH - 2:
+                permute_some(k + 2, range(3, 4), SCALAR)
             matmul_mx(second)
             forget(first)
             cell(first, GPSIMD)

from contextlib import ExitStack

import concourse.mybir as mybir
from concourse.masks import make_identity

F32 = mybir.dt.float32
BF16 = mybir.dt.bfloat16
U32 = mybir.dt.uint32
U8 = mybir.dt.uint8
I32 = mybir.dt.int32
FP8X4 = mybir.dt.float8_e4m3fn_x4
ACT = mybir.ActivationFunctionType
ALU = mybir.AluOpType

P = 128
B, T, I, H = 128, 8, 1024, 1024
NG = 4
NCH = H // P
RAW_BUFS = 12
VECTOR, SCALAR, GPSIMD = 0, 1, 2
COPY_X_HEAD = (VECTOR, SCALAR)
COPY_X = (VECTOR, VECTOR)
COPY_I = (SCALAR, SCALAR, SCALAR, SCALAR)
COPY_I_HEAD = (VECTOR, SCALAR, VECTOR, SCALAR)
COPY_H = (SCALAR, SCALAR, SCALAR, SCALAR)
COPY_H_HEAD = (SCALAR, VECTOR, SCALAR, VECTOR)
UNITS = [(k, t0, 4) for k in range(NCH - 1) for t0 in (0, 4)]
TAIL = [(NCH - 1, 0, 2), (NCH - 1, 2, 2), (NCH - 1, 4, 2), (NCH - 1, 6, 2)]

FLOPS = 2 * B * T * I * NG * H + 2 * B * H * NG * H


def tile_naivelstm_pa_kernel(
    tc,
    inputs, h0, c0,
    w_ii, b_ii, w_hi, b_hi,
    w_if_, b_if_, w_hf, b_hf,
    w_io, b_io, w_ho, b_ho,
    w_ig, b_ig, w_hg, b_hg,
    out_0, out_1, out_2,
):
    nc = tc.nc
    w_in = [w_ii, w_if_, w_io, w_ig]
    w_hid = [w_hi, w_hf, w_ho, w_hg]
    b_in = [b_ii, b_if_, b_io, b_ig]
    b_hid = [b_hi, b_hf, b_ho, b_hg]

    with ExitStack() as ctx:
        ctx.enter_context(tc.manual_schedule())
        const = ctx.enter_context(tc.tile_pool(name="const", bufs=1))
        raw = ctx.enter_context(tc.tile_pool(name="raw", bufs=RAW_BUFS))
        rawq = ctx.enter_context(tc.tile_pool(name="rawq", bufs=2))
        wgp = ctx.enter_context(tc.tile_pool(name="wgp", bufs=2))
        wqp = ctx.enter_context(tc.tile_pool(name="wqp", bufs=3))
        whp = ctx.enter_context(tc.tile_pool(name="whp", bufs=2))
        zp = ctx.enter_context(tc.tile_pool(name="zp", bufs=6))
        perm = ctx.enter_context(tc.tile_pool(name="perm", bufs=4))
        hp = ctx.enter_context(tc.tile_pool(name="hp", bufs=6))
        psum = ctx.enter_context(tc.psum_pool(name="psum", bufs=7))
        psum_c0 = ctx.enter_context(tc.psum_pool(name="psum_c0", bufs=1))

        ident = const.tile([P, P], F32, name="ident")
        ident_bf = const.tile([P, P], BF16, name="ident_bf")
        ones = const.tile([P, P], BF16, name="ones")
        scratch = const.tile([P, 1], F32, name="scratch")
        bias_sb = const.tile([P, NCH, NG, P], BF16, name="bias_sb")
        h0_raw = const.tile([P, H], BF16, name="h0_raw")
        c0_sb = const.tile([P, H], BF16, name="c0_sb")
        h_t = const.tile([P, 4, 2, P], BF16, name="h_t")
        h0_perm = const.tile([P, H], BF16, name="h0_perm")
        h_tq = const.tile([P, 4, 2, P], BF16, name="h_tq")
        x_raw = const.tile([P, T, I], BF16, name="x_raw")
        xg = const.tile([P, T, I], BF16, name="xg", align_bytes=64)
        xq = const.tile([P, T, I // 4], U32, name="xq", align_bytes=64)
        xs = const.tile([P, T, I // 4], U8, name="xs", align_bytes=64)
        gsum = const.tile([P, NCH, NG * P], F32, name="gsum")

        nc.vector.memset(bias_sb[:].bitcast(I32), 0)
        make_identity(nc, ident[:])
        nc.vector.memset(scratch[:], 0.0)
        nc.vector.memset(ones[:], 1.0)

        raw_tiles = {}
        in_order = [("H", 0), ("I", 0), ("H", 1)] + [("I", k) for k in range(1, NCH)]
        whole = [(kind, k, g) for kind, k in in_order for g in range(NG)]
        cursor = [0]

        def load_rows():
            n = cursor[0]
            if n < len(whole):
                kind, k, g = whole[n]
                w = w_hid[g] if kind == "H" else w_in[g]
                wraw = raw.tile([P, I], BF16, name="wraw", tag="wraw")
                nc.sync.dma_start(out=wraw[:], in_=w[k * P:(k + 1) * P, :])
                raw_tiles[whole[n]] = wraw
                cursor[0] = n + 1

        def load_quadrants(k):
            if k < NCH:
                wraw = rawq.tile([P, NG, 4, 256], BF16, name="wrawq", align_bytes=64)
                for g in range(NG):
                    for q in (0, 2, 1, 3):
                        nc.sync.dma_start(
                            out=wraw[32 * q:32 * (q + 1), g, :, :],
                            in_=w_hid[g][k * P:(k + 1) * P, 256 * q:256 * (q + 1)].rearrange(
                                "(m r) e -> r m e", r=32
                            ),
                        )
                raw_tiles[("Q", k)] = wraw

        nc.sync.dma_start(out=h0_raw[:], in_=h0[0])
        for g in range(NG):
            nc.scalar.dma_start(
                out=bias_sb[0:1, :, g, :],
                in_=b_in[g].rearrange("(k r) o -> o k r", r=P),
            )
            nc.gpsimd.dma_start(
                out=bias_sb[1:2, :, g, :],
                in_=b_hid[g].rearrange("(k r) o -> o k r", r=P),
            )
        nc.scalar.activation(out=scratch[:], in_=scratch[:], func=ACT.Sigmoid)
        nc.gpsimd.dma_start(out=c0_sb[:], in_=c0[0])
        make_identity(nc, ident_bf[:])
        def load_x(pair):
            tt = slice(2 * pair, 2 * pair + 2)
            nc.sync.dma_start(out=x_raw[:, tt, :], in_=inputs[:, tt, :])

        for g in range(NG):
            load_rows()
        load_x(0)
        load_x(1)
        for g in range(NG):
            load_rows()
        load_x(2)
        load_x(3)
        for g in range(NG):
            load_rows()

        def copy(engine, out, in_):
            if engine == VECTOR:
                nc.vector.tensor_copy(out=out, in_=in_)
            else:
                nc.scalar.copy(out=out, in_=in_)

        def transpose_words(words):
            bank = psum.tile([P, 4, P], F32, name="tp", tag="bank")
            for q in range(4):
                nc.tensor.transpose(bank[:, q, :], words[:, q * P:(q + 1) * P], ident[:])
            return bank

        def transpose_for_mx(words):
            bank = psum.tile([P, 4, P], F32, name="tp", tag="bank")
            for g in range(2):
                for u in range(2):
                    nc.tensor.transpose(
                        bank[:, 2 * g + u, :], words[:, 256 * g + u:256 * (g + 1):2], ident[:]
                    )
            return bank

        def permuted(words):
            tile = perm.tile([P, I // 2], F32, name="perm")
            nc.vector.tensor_copy(
                out=tile[:].rearrange("p (g u w) -> p g u w", g=2, u=2),
                in_=words.rearrange("p (g w u) -> p g u w", g=2, u=2),
            )
            return tile[:]

        def regrouped(bank):
            return bank[:].rearrange("p (g u) r -> p g r u", u=2)

        permuted_tiles = {}
        in_banks = {}
        wh_tiles = {}
        wg_tiles = {}
        wq_tiles = {}
        banks_of = {}
        z_tiles = {}
        c0_banks = {}

        def prepare_h0():
            bank = transpose_words(h0_raw[:].bitcast(F32))
            nc.vector.tensor_copy(
                out=h_t[:],
                in_=bank[:].bitcast(BF16).rearrange("p j (b e) -> p j e b", e=2),
            )

        def permute_x(pair):
            for t in (2 * pair, 2 * pair + 1):
                permuted_tiles[("x", t)] = permuted(x_raw[:].bitcast(F32)[:, t, :])

        def permute_in(k):
            for g in range(NG):
                permuted_tiles[(k, g)] = permuted(raw_tiles[("I", k, g)][:].bitcast(F32))

        def permute_some(k, gates, engine):
            for g in gates:
                tile = perm.tile([P, I // 2], F32, name="perm")
                copy(
                    engine,
                    tile[:].rearrange("p (g u w) -> p g u w", g=2, u=2),
                    raw_tiles[("I", k, g)][:].bitcast(F32).rearrange("p (g w u) -> p g u w", g=2, u=2),
                )
                permuted_tiles[(k, g)] = tile[:]

        def transpose_x(pair, engines):
            for n in range(2):
                t = 2 * pair + n
                if ("x", t) in permuted_tiles:
                    bank = transpose_words(permuted_tiles[("x", t)])
                else:
                    bank = transpose_for_mx(x_raw[:].bitcast(F32)[:, t, :])
                copy(
                    engines[n],
                    xg[:].bitcast(F32)[:, 2 * pair + n, :].rearrange(
                        "p (g r u) -> p g r u", g=2, u=2
                    ),
                    regrouped(bank),
                )

        def quantise_x(pair):
            tt = slice(2 * pair, 2 * pair + 2)
            nc.vector.quantize_mx(
                out=xq[:, tt, :].rearrange("p t c -> p (t c)").bitcast(FP8X4),
                scales=xs[:, tt, :].rearrange("p t c -> p (t c)"),
                in_=xg[:, tt, :].rearrange("p t c -> p (t c)"),
            )

        def prepare_h0_quadrants():
            nc.vector.tensor_copy(
                out=h0_perm[:].rearrange("p (j q c) -> p j q c", j=4, q=4),
                in_=h0_raw[:].rearrange("p (q j c) -> p j q c", j=4, q=4),
            )
            bank = transpose_words(h0_perm[:].bitcast(F32))
            nc.scalar.copy(
                out=h_tq[:],
                in_=bank[:].bitcast(BF16).rearrange("p j (b e) -> p j e b", e=2),
            )

        def transpose_quadrants(k, part):
            if part == 0:
                wh_tiles[k] = whp.tile([P, 4, NG * P], F32, name="wh_t", align_bytes=64)
            gg = slice(2 * part, 2 * part + 2)
            nc.vector.transpose(
                out=wh_tiles[k][:, gg, :].rearrange("p g c -> p (g c)"),
                in_=raw_tiles[("Q", k)][:, gg, :, :].rearrange("p g m e -> p (g m e)").bitcast(F32),
            )
            if part == 1:
                load_quadrants(k + 2)

        def transpose_hid(k):
            banks = []
            for g in range(NG):
                banks.append(transpose_words(raw_tiles[("H", k, g)][:].bitcast(F32)))
                load_rows()
            banks_of["H"] = banks

        def copy_hid(k, engines):
            wh_t = whp.tile([P, 4, NG * P], F32, name="wh_t", align_bytes=64)
            wh_tiles[k] = wh_t
            for g in range(NG):
                copy(engines[g], wh_t[:, :, g * P:(g + 1) * P], banks_of["H"][g][:])

        def matmul_hid(k):
            bank = psum.tile([P, NG * P], F32, name="hid", tag="bank")
            if k < 2:
                wv = wh_tiles[k][:].bitcast(BF16).rearrange("p j (c e) -> p j e c", e=2)
                out, ht = bank[:], h_t
            else:
                wv = wh_tiles[k][:].bitcast(BF16).rearrange(
                    "p g (m j r e) -> p j e (g m) r", m=4, j=4, e=2
                )
                out, ht = bank[:].rearrange("p (m r) -> p m r", r=32), h_tq
            for j in range(4):
                for e in range(2):
                    nc.tensor.matmul(
                        out, lhsT=ht[:, j, e, :], rhs=wv[:, j, e],
                        start=(j == 0 and e == 0), stop=False,
                    )
            nc.tensor.matmul(
                bank[:], lhsT=ones[:],
                rhs=bias_sb[:, k, :, :].rearrange("p g r -> p (g r)"),
                start=False, stop=True,
            )
            nc.scalar.copy(out=gsum[:, k, :], in_=bank[:])

        def transpose_in(k, gates=range(NG)):
            for g in gates:
                if (k, g) in permuted_tiles:
                    bank = transpose_words(permuted_tiles[(k, g)])
                else:
                    bank = transpose_for_mx(raw_tiles[("I", k, g)][:].bitcast(F32))
                in_banks[(k, g)] = bank
                load_rows()

        def copy_in(k, engines, gates=range(NG)):
            if k not in wg_tiles:
                wg_tiles[k] = wgp.tile([P, 2, NG, 4 * P], BF16, name="wg", align_bytes=64)
            for g in gates:
                copy(
                    engines[g],
                    wg_tiles[k][:].bitcast(F32)[:, :, g, :].rearrange("p g (r u) -> p g r u", u=2),
                    regrouped(in_banks[(k, g)]),
                )

        def quantise_in(k):
            wq = wqp.tile([P, 2, NG * P], U32, name="wq", align_bytes=64)
            ws = wqp.tile([P, 2, NG * P], U8, name="ws", align_bytes=64)
            wq_tiles[k] = (wq, ws)
            nc.vector.quantize_mx(
                out=wq[:].rearrange("p g c -> p (g c)").bitcast(FP8X4),
                scales=ws[:].rearrange("p g c -> p (g c)"),
                in_=wg_tiles[k][:].rearrange("p g n c -> p (g n c)"),
            )

        def load_c0_bank(j):
            bank = psum_c0.tile([P, 4 * P], F32, name="c0_bank")
            nc.tensor.matmul(
                bank[:], lhsT=ident_bf[:], rhs=c0_sb[:, 4 * j * P:4 * (j + 1) * P],
                start=True, stop=True,
            )
            c0_banks[j] = bank

        def matmul_mx(u):
            chunk, t0, nt = u
            wq, ws = wq_tiles[chunk]
            z = zp.tile([P, NG, nt, P], F32, name="z")
            z_tiles[u] = z
            for tl in range(nt):
                t = t0 + tl
                bank = psum.tile([P, NG, P], F32, name="mx", tag="bank")
                for g in range(2):
                    cols = slice(g * P, (g + 1) * P)
                    nc.tensor.matmul_mx(
                        out=bank[:].rearrange("p g r -> p (g r)"),
                        lhsT=xq[:, t, cols].bitcast(FP8X4),
                        lhsT_scale=xs[:, t, cols],
                        rhs=wq[:, g, :].bitcast(FP8X4),
                        rhs_scale=ws[:, g, :],
                        start=(g == 0),
                        stop=(g == 1),
                    )
                nc.vector.tensor_tensor(
                    out=z[:, :, tl, :],
                    in0=bank[:],
                    in1=gsum[:, chunk, :].rearrange("p (g r) -> p g r", g=NG),
                    op=ALU.add,
                )

        def product(engine, out, in0, in1, op):
            if engine == VECTOR:
                nc.vector.tensor_tensor(out=out, in0=in0, in1=in1, op=op)
            else:
                nc.gpsimd.tensor_tensor(out=out, in0=in0, in1=in1, op=op)

        def sigmoid_gates(u):
            sig = z_tiles[u][:, 0:3, :, :].rearrange("p g t r -> p (g t r)")
            nc.scalar.activation(out=sig, in_=sig, func=ACT.Sigmoid)

        def tanh_gate(u):
            z = z_tiles[u]
            nc.scalar.activation(out=z[:, 3], in_=z[:, 3], func=ACT.Tanh)

        def forget(u):
            chunk, t0, nt = u
            z = z_tiles[u]
            c0_view = c0_banks[chunk // 4][:, (chunk % 4) * P:(chunk % 4 + 1) * P]
            nc.vector.tensor_tensor(
                out=z[:, 1], in0=z[:, 1],
                in1=c0_view.unsqueeze(1).to_broadcast([P, nt, P]),
                op=ALU.mult,
            )

        def update(u, engine):
            z = z_tiles[u]
            product(engine, z[:, 0], z[:, 0], z[:, 3], ALU.mult)

        def cell(u, engine):
            z = z_tiles[u]
            product(engine, z[:, 3], z[:, 0], z[:, 1], ALU.add)

        def tanh_cell(u):
            z = z_tiles[u]
            nc.scalar.activation(out=z[:, 1], in_=z[:, 3], func=ACT.Tanh)

        def store(u, engine):
            chunk, t0, nt = u
            ks = slice(chunk * P, (chunk + 1) * P)
            z = z_tiles[u]
            hout = hp.tile([P, nt, P], F32, name="hout")
            product(engine, hout[:], z[:, 2], z[:, 1], ALU.mult)
            if t0 + nt == T:
                nc.sync.dma_start(out=out_2[0, :, ks], in_=z[:, 3, nt - 1, :])
            nc.sync.dma_start(
                out=out_0[t0:t0 + nt, :, ks].rearrange("t b h -> b t h"), in_=hout[:]
            )
            if t0 + nt == T:
                nc.sync.dma_start(out=out_1[0, :, ks], in_=hout[:, nt - 1, :])

        prepare_h0()
        prepare_h0_quadrants()
        transpose_hid(0)
        load_quadrants(2)
        copy_hid(0, COPY_H_HEAD)
        transpose_x(0, COPY_X_HEAD)
        transpose_x(1, COPY_X_HEAD)
        quantise_x(0)
        transpose_in(0)
        load_quadrants(3)
        copy_in(0, COPY_I_HEAD)
        quantise_x(1)
        matmul_hid(0)
        quantise_in(0)
        permute_x(2)
        permute_x(3)

        older, previous = UNITS[0], UNITS[1]
        matmul_mx(older)
        transpose_x(2, COPY_X_HEAD)
        transpose_x(3, COPY_X_HEAD)
        permute_in(1)
        quantise_x(2)
        transpose_hid(1)
        copy_hid(1, COPY_H)
        quantise_x(3)
        transpose_in(1)
        copy_in(1, COPY_I)
        transpose_quadrants(2, 0)
        quantise_in(1)
        sigmoid_gates(older)
        tanh_gate(older)
        matmul_mx(previous)
        matmul_hid(1)
        update(older, GPSIMD)
        transpose_quadrants(2, 1)
        load_c0_bank(0)
        forget(older)
        cell(older, GPSIMD)
        sigmoid_gates(previous)
        tanh_gate(previous)
        update(previous, GPSIMD)

        for k in range(1, NCH - 2):
            first, second = UNITS[2 * k], UNITS[2 * k + 1]
            matmul_mx(first)
            forget(previous)
            cell(previous, GPSIMD)
            transpose_in(k + 1)
            copy_in(k + 1, COPY_I)
            transpose_quadrants(k + 2, 0)
            transpose_quadrants(k + 2, 1)
            quantise_in(k + 1)
            tanh_cell(older)
            store(older, GPSIMD)
            sigmoid_gates(first)
            tanh_gate(first)
            matmul_hid(k + 1)
            if k == 4:
                load_c0_bank(1)
            tanh_cell(previous)
            update(first, GPSIMD)
            store(previous, GPSIMD)
            if k < NCH - 2:
                permute_some(k + 2, range(3, 4), SCALAR)
            matmul_mx(second)
            forget(first)
            cell(first, GPSIMD)
            sigmoid_gates(second)
            tanh_gate(second)
            update(second, GPSIMD)
            older = first
            previous = second

        last = NCH - 1
        first, second = UNITS[2 * last - 2], UNITS[2 * last - 1]
        matmul_mx(first)
        forget(previous)
        matmul_mx(second)
        transpose_in(last)
        sigmoid_gates(first)
        copy_in(last, (SCALAR, SCALAR, SCALAR, SCALAR))
        tanh_gate(first)
        forget(first)
        cell(previous, VECTOR)
        quantise_in(last)
        sigmoid_gates(second)
        tanh_gate(second)
        matmul_hid(last)
        update(first, VECTOR)
        forget(second)
        cell(first, VECTOR)
        tanh_cell(older)
        update(second, VECTOR)
        store(older, GPSIMD)
        matmul_mx(TAIL[0])
        cell(second, VECTOR)
        tanh_cell(previous)
        store(previous, GPSIMD)
        sigmoid_gates(TAIL[0])
        tanh_gate(TAIL[0])
        matmul_mx(TAIL[1])
        tanh_cell(first)
        store(first, GPSIMD)
        sigmoid_gates(TAIL[1])
        tanh_gate(TAIL[1])
        matmul_mx(TAIL[2])
        tanh_cell(second)
        sigmoid_gates(TAIL[2])
        tanh_gate(TAIL[2])
        matmul_mx(TAIL[3])
        store(second, GPSIMD)
        forget(TAIL[0])
        forget(TAIL[1])
        update(TAIL[0], VECTOR)
        update(TAIL[1], VECTOR)
        cell(TAIL[0], VECTOR)
        cell(TAIL[1], VECTOR)
        sigmoid_gates(TAIL[3])
        tanh_gate(TAIL[3])
        forget(TAIL[2])
        tanh_cell(TAIL[0])
        tanh_cell(TAIL[1])
        update(TAIL[2], VECTOR)
        forget(TAIL[3])
        cell(TAIL[2], VECTOR)
        update(TAIL[3], VECTOR)
        store(TAIL[0], VECTOR)
        cell(TAIL[3], VECTOR)
        tanh_cell(TAIL[2])
        store(TAIL[1], VECTOR)
        tanh_cell(TAIL[3])
        store(TAIL[2], VECTOR)
        store(TAIL[3], VECTOR)
